import numpy as np
import ml_dtypes


def mxq(x, axis, fmt="e4m3"):
    dtype, down = {"e4m3": (ml_dtypes.float8_e4m3fn, 7), "e5m2": (ml_dtypes.float8_e5m2, 14)}[fmt]
    v = np.moveaxis(np.asarray(x, np.float32).astype(ml_dtypes.bfloat16).astype(np.float64), axis, -1)
    blocks = v.reshape(v.shape[:-1] + (-1, 32))
    amax = np.abs(blocks).max(-1, keepdims=True)
    byte = np.maximum(np.where(amax > 0, np.frexp(amax)[1] - 1 + 127, 0) - down, 1)
    scale = np.exp2(byte - 127.0)
    codes = (blocks / scale).astype(np.float32).astype(dtype).astype(np.float64)
    return np.moveaxis((codes * scale).reshape(v.shape), -1, axis)


WIDE = False


def mx_kscale(k):
    if not WIDE:
        return np.ones(k)
    levels = np.array([10, -10, 5, -5, 0])
    if k % 512:
        return np.exp2(np.random.permutation(np.resize(levels, k // 32))).repeat(32)
    a = np.empty((k // 512, 16))
    for p in range(k // 512):
        a[p, :8] = np.random.permutation(np.resize(levels, 8))
        for g in range(8):
            far = levels[np.abs(levels - a[p, g]) >= 10]
            a[p, g + 8] = far[np.random.randint(len(far))]
    return np.exp2(a.ravel()).repeat(32)


BF16 = ml_dtypes.bfloat16


def bf(x):
    return np.asarray(x, np.float32).astype(BF16)


def f64(x):
    return np.asarray(x).astype(np.float64)


B, T, C, NH, NC = 2, 2048, 512, 4, 2
HS = C // NH
N = T // NC


def draw0():
    s = mx_kscale(C)
    t = mx_kscale(T)
    return {"x": bf(np.random.standard_normal((B, T, C)) * s * t[:, None]),
            "Wk": bf(np.random.standard_normal((C, C)) / np.sqrt(C) / s),
            "pk_W": bf(np.random.standard_normal((NC, N, N)) / np.sqrt(N) / t.reshape(NC, 1, N)),
            "pk_b": bf(np.random.standard_normal((NC, N)) * 0.3)}


def core(x, Wk, pk_W, pk_b):
    kh = mxq(f64(x), 2, "e4m3") @ mxq(f64(Wk), 1, "e4m3").T
    kh = kh.reshape(B, T, NH, HS).transpose(0, 2, 1, 3).reshape(B, NH, NC, N, HS)
    out = (mxq(f64(pk_W), 2, "e4m3") @ mxq(kh, 3, "e4m3")) + f64(pk_b)[:, :, None]
    return out.reshape(B, NH, T, HS)


def e4m3fn_bytes(y):
    return np.clip(np.asarray(y, np.float64), -448.0, 448.0).astype(np.float32).astype(ml_dtypes.float8_e4m3fn).view(np.uint8)


def e4m3fn_values(b):
    return np.asarray(b, np.uint8).view(ml_dtypes.float8_e4m3fn).astype(np.float64)


def setup_inputs():
    d = draw0()
    x0 = np.asarray(d['Wk']).astype(np.float64)
    s = (np.max(np.abs(x0), axis=(0,), keepdims=True) / 448.0).astype(np.float32)
    out = {}
    for k, v in d.items():
        if k == 'Wk':
            out['Wk_bytes'] = e4m3fn_bytes(x0 / s.astype(np.float64))
            out['Wk_scale'] = s
        else:
            out[k] = v
    return out


def reference(x, Wk_bytes, Wk_scale, pk_W, pk_b):
    return core(x, e4m3fn_values(Wk_bytes) * Wk_scale.astype(np.float64), pk_W, pk_b)

@@ -1,0 +1,309 @@
+from contextlib import ExitStack
+
+import concourse.mybir as mybir
+from concourse.masks import make_identity
+
+B, T, C, NH, NC = 2, 2048, 512, 4, 2
+D = C // NH
+N = T // NC
+FLOPS = 2 * B * T * C * C + 2 * B * T * N * C
+
+F32 = mybir.dt.float32
+BF16 = mybir.dt.bfloat16
+U32 = mybir.dt.uint32
+U8 = mybir.dt.uint8
+FP8 = mybir.dt.float8_e4m3fn
+FP8X4 = mybir.dt.float8_e4m3fn_x4
+ADD = mybir.AluOpType.add
+MULT = mybir.AluOpType.mult
+IDENT = mybir.ActivationFunctionType.Identity
+P = 128
+
+EVAC = {"t": "SVS", "s": "SSSV", "o": "SSVSSSV"}
+QDELAY = 3
+LEAD = 10
+DEINT_X = [6,7]
+DEINT_P = [8,9,10,11,12,13,14,15]
+DEINT_ENGINE = "V"
+
+
+def build_schedule():
+    def xj(i):
+        return [("X", i, 0), ("X", i, 1)]
+
+    def pj(c, js):
+        return [("P", c, j) for j in js]
+
+    def sj(i, hs=(0, 1, 2, 3)):
+        return [("S", i, h) for h in hs]
+
+    def oj(pair, js):
+        return [("O", pair, j) for j in js]
+
+    w = [("W", 0, 0), ("W", 1, 0)]
+    return (
+        xj(0) + w + pj(0, [0, 1]) + pj(0, [2, 3]) + pj(0, [4, 5]) + xj(1)
+        + pj(0, [6, 7]) + xj(2) + xj(3) + sj(0) + xj(4) + sj(1)
+        + sj(2) + xj(5) + oj(0, [0, 1]) + sj(3) + oj(0, [2, 3]) + sj(4)
+        + pj(1, [0, 1]) + oj(0, [4, 5]) + oj(0, [6, 7]) + sj(5, [0, 1]) + oj(1, [0, 1]) + xj(6)
+        + xj(7) + oj(1, [2, 3]) + sj(5, [2, 3]) + oj(1, [4, 5]) + pj(1, [2, 3]) + pj(1, [4, 5])
+        + sj(6, [0, 1]) + oj(1, [6, 7]) + oj(2, [0, 1]) + oj(2, [2, 3]) + sj(6, [2, 3]) + pj(1, [6, 7])
+        + sj(7) + oj(2, [4, 5]) + oj(2, [6, 7]) + oj(3, [0, 1]) + oj(3, [2, 3]) + oj(3, [4, 5])
+        + oj(3, [6, 7])
+    )
+
+
+def tile_causalselfattention_pa_t_kernel(tc, x, wk_bytes, wk_scale, pk_w, pk_b, out):
+    nc = tc.nc
+    with ExitStack() as ctx:
+        keep = ctx.enter_context(tc.tile_pool(name="keep", bufs=1))
+        work = ctx.enter_context(tc.tile_pool(name="work", bufs=3))
+        psum = ctx.enter_context(tc.psum_pool(name="psum", bufs=8))
+        ctx.enter_context(tc.manual_schedule())
+
+        wb = keep.tile([P, 4, C], U8, name="wb", align_bytes=64)
+        nc.sync.dma_start(out=wb[:], in_=wk_bytes.rearrange("(i r) k -> r i k", r=P))
+        ws = keep.tile([P, 4], F32, name="ws", align_bytes=64)
+        nc.scalar.dma_start(out=ws[:], in_=wk_scale.rearrange("o (p t) -> p (o t)", t=4))
+
+        xraw = {}
+        praw = {}
+
+        def load_x(i, pieces):
+            pair, u = divmod(i, 2)
+            c, b = divmod(pair, 2)
+            r0 = c * N + u * 512
+            t = keep.tile([P, 4, C], BF16, name="xraw%d" % i, align_bytes=64)
+            src = x[b, r0:r0 + 512, :].rearrange("(m t) k -> m t k", t=4)
+            n = 4 // pieces
+            for s in range(pieces):
+                nc.sync.dma_start(out=t[:, s * n:(s + 1) * n, :], in_=src[:, s * n:(s + 1) * n, :])
+            xraw[i] = t
+
+        def load_p(c, q, half):
+            if (c, q) not in praw:
+                praw[(c, q)] = keep.tile([P, 4, N], BF16, name="praw%d%d" % (c, q), align_bytes=64)
+            src = pk_w[c, q * 512:(q + 1) * 512, :].rearrange("(m j) k -> m j k", j=4)
+            rows = slice(2 * half, 2 * half + 2)
+            nc.sync.dma_start(out=praw[(c, q)][:, rows, :], in_=src[:, rows, :])
+
+        load_x(0, 2)
+        bias_bf = keep.tile([P, 4, 4], BF16, name="bias_bf", align_bytes=64)
+        bias = keep.tile([P, 16], F32, name="bias", align_bytes=64)
+        load_p(0, 0, 0)
+        load_p(0, 0, 1)
+        load_p(0, 1, 0)
+        load_x(1, 1)
+        load_p(0, 1, 1)
+        load_x(2, 1)
+        load_x(3, 1)
+        load_x(4, 1)
+        load_x(5, 1)
+        load_p(1, 0, 0)
+        load_x(6, 1)
+        nc.sync.dma_start(out=bias_bf[:], in_=pk_b.rearrange("c (q p j) -> p (c q) j", q=2, j=4))
+        load_x(7, 1)
+        load_p(1, 0, 1)
+        load_p(1, 1, 0)
+        load_p(1, 1, 1)
+
+        warm = keep.tile([P, 1], F32, name="warm")
+        warm2 = keep.tile([P, 1], F32, name="warm2")
+        nc.vector.memset(warm[:], 0.0)
+        nc.scalar.activation(out=warm2[:], in_=warm[:], func=IDENT)
+        ident = keep.tile([P, P], F32, name="ident", align_bytes=64)
+        make_identity(nc, ident[:])
+        nc.gpsimd.tensor_copy(out=bias[:], in_=bias_bf[:].rearrange("p a j -> p (a j)"))
+
+        wv = keep.tile([P, 4, C], BF16, name="wv", align_bytes=64)
+        nc.vector.tensor_copy(out=wv[:, 0:2, :].rearrange("p i k -> p (i k)"),
+                              in_=wb[:, 0:2, :].rearrange("p i k -> p (i k)").bitcast(FP8))
+        nc.scalar.copy(out=wv[:, 2:4, :].rearrange("p i k -> p (i k)"),
+                       in_=wb[:, 2:4, :].rearrange("p i k -> p (i k)").bitcast(FP8))
+
+        wg = keep.tile([P, C * 4], BF16, name="wg", align_bytes=64)
+        wcodes = keep.tile([P, C], U32, name="wcodes", align_bytes=64)
+        wscales = keep.tile([P, C], U8, name="wscales", align_bytes=64)
+
+        xcodes, xscales, pcodes, pscales, kcodes, kscales, otiles = {}, {}, {}, {}, {}, {}, {}
+        grouped = {}
+        due = []
+        count = [0, 0]
+        evac_count = {}
+        words = {}
+
+        def evac_engine(kind):
+            n = evac_count.get(kind, 0)
+            evac_count[kind] = n + 1
+            return EVAC[kind][n % len(EVAC[kind])]
+
+        def copy_out(kind, out_, in_):
+            if evac_engine(kind) == "S":
+                nc.scalar.copy(out=out_, in_=in_)
+            else:
+                nc.vector.tensor_copy(out=out_, in_=in_)
+
+        def later(fn, delay=QDELAY):
+            due.append((count[0] + delay, fn))
+
+        def quant(codes, scales, src):
+            nc.vector.quantize_mx(out=codes[:].bitcast(FP8X4), scales=scales[:], in_=src[:])
+
+        def raw_words(kind, i, a):
+            if kind == "X":
+                return xraw[i][:, 2 * a:2 * a + 2, :].rearrange("p s k -> p (s k)").bitcast(F32)
+            return praw[(i, a // 4)][:, a % 4, :].bitcast(F32)
+
+        def deinterleave(job):
+            kind = job[0]
+            if job in words:
+                return
+            if (kind == "X" and job[1] in DEINT_X) or (kind == "P" and (job[1] * 8 + job[2]) in DEINT_P):
+                d = work.tile([P, 4, P], F32, name="deint", bufs=10, align_bytes=64)
+                eng = nc.vector if DEINT_ENGINE == "V" else nc.gpsimd
+                eng.tensor_copy(out=d[:].rearrange("p (g u) m -> p g u m", g=2),
+                                in_=raw_words(*job).rearrange("p (g m u) -> p g u m", g=2, u=2))
+                words[job] = [d[:, n, :] for n in range(4)]
+            elif kind in ("X", "P"):
+                r = raw_words(*job)
+                words[job] = [r[:, 256 * g + u:256 * (g + 1):2] for g in range(2) for u in range(2)]
+
+        def bank(name):
+            return psum.tile([P, 512], F32, name="bank")
+
+        def turn(job, dst):
+            bk = bank("t")
+            for n in range(4):
+                nc.tensor.transpose(bk[:, n * P:(n + 1) * P], words[job][n], ident[:])
+            copy_out("t", dst.bitcast(F32).rearrange("p (g m u) -> p g m u", g=2, u=2),
+                     bk[:].rearrange("p (g u m) -> p g m u", g=2, u=2))
+
+        def do_w(a):
+            bk = bank("w")
+            for i2 in range(2):
+                ww = wv[:, 2 * a + i2, :].bitcast(F32)
+                for u in range(2):
+                    n = 2 * i2 + u
+                    nc.tensor.transpose(bk[:, n * P:(n + 1) * P], ww[:, u:256:2], ident[:])
+            vals = bk[:].bitcast(BF16)
+            for i2 in range(2):
+                base = (2 * a + i2) * 512
+                nc.vector.tensor_tensor(
+                    out=wg[:, base:base + 512].rearrange("p (r u e) -> p r u e", u=2, e=2),
+                    in0=vals[:, i2 * 512:(i2 + 1) * 512].rearrange("p (u r e) -> p r u e", u=2, e=2),
+                    in1=ws[:].rearrange("p (u e) -> p u e", u=2).unsqueeze(1).to_broadcast([P, P, 2, 2]),
+                    op=MULT)
+            later(lambda: nc.vector.quantize_mx(
+                out=wcodes[:, a * 256:(a + 1) * 256].bitcast(FP8X4),
+                scales=wscales[:, a * 256:(a + 1) * 256],
+                in_=wg[:, a * 1024:(a + 1) * 1024]), 1)
+
+        def do_x(i, a):
+            if a == 0:
+                grouped[("X", i)] = work.tile([P, 2048], BF16, name="xg", align_bytes=64)
+            g = grouped[("X", i)]
+            turn(("X", i, a), g[:, a * 1024:(a + 1) * 1024])
+            if a == 1:
+                xcodes[i] = work.tile([P, C], U32, name="xcodes", bufs=6, align_bytes=64)
+                xscales[i] = work.tile([P, C], U8, name="xscales", bufs=6, align_bytes=64)
+                later(lambda: quant(xcodes[i], xscales[i], g))
+
+        def do_p(c, j):
+            key = (c, j // 2)
+            if j % 2 == 0:
+                grouped[("P",) + key] = work.tile([P, 2048], BF16, name="pg", align_bytes=64)
+            g = grouped[("P",) + key]
+            turn(("P", c, j), g[:, (j % 2) * 1024:(j % 2 + 1) * 1024])
+            if j % 2 == 1:
+                pcodes[key] = keep.tile([P, 512], U32, name="pcodes%d%d" % key, align_bytes=64)
+                pscales[key] = keep.tile([P, 512], U8, name="pscales%d%d" % key, align_bytes=64)
+                later(lambda: quant(pcodes[key], pscales[key], g))
+
+        def do_s(i, h):
+            if h == 0:
+                grouped[("K", i)] = work.tile([P, 2048], BF16, name="kg", align_bytes=64)
+            g = grouped[("K", i)]
+            bk = bank("s")
+            for t in range(4):
+                nc.tensor.matmul_mx(
+                    out=bk[:, t * P:(t + 1) * P],
+                    lhsT=xcodes[i][:, t * P:(t + 1) * P].bitcast(FP8X4),
+                    lhsT_scale=xscales[i][:, t * P:(t + 1) * P],
+                    rhs=wcodes[:, h * P:(h + 1) * P].bitcast(FP8X4),
+                    rhs_scale=wscales[:, h * P:(h + 1) * P],
+                    start=True, stop=True)
+            copy_out("s", g[:, h * 512:(h + 1) * 512].rearrange("p (n t) -> p n t", t=4),
+                     bk[:].rearrange("p (t n) -> p n t", t=4))
+            if h == 3:
+                kcodes[i] = work.tile([P, C], U32, name="kcodes", bufs=8, align_bytes=64)
+                kscales[i] = work.tile([P, C], U8, name="kscales", bufs=8, align_bytes=64)
+                later(lambda: quant(kcodes[i], kscales[i], g))
+
+        def do_o(pair, j):
+            c, b = divmod(pair, 2)
+            q, jj = divmod(j, 4)
+            if jj == 0:
+                otiles[(pair, q)] = work.tile([P, NH, 4, D], F32, name="o", align_bytes=64)
+            o = otiles[(pair, q)]
+            bk = bank("o")
+            s0 = (j % 2) * 256
+            key = (c, j // 2)
+            for u in range(2):
+                cols = slice(s0 + u * P, s0 + (u + 1) * P)
+                nc.tensor.matmul_mx(
+                    out=bk[:],
+                    lhsT=pcodes[key][:, cols].bitcast(FP8X4),
+                    lhsT_scale=pscales[key][:, cols],
+                    rhs=kcodes[2 * pair + u][:].bitcast(FP8X4),
+                    rhs_scale=kscales[2 * pair + u][:],
+                    start=(u == 0), stop=(u == 1))
+            bcol = bias[:, (2 * c + q) * 4 + jj:(2 * c + q) * 4 + jj + 1]
+            src = bk[:].rearrange("p (h d) -> p h d", h=NH)
+            last = pair == 3 and j == 7
+
+            def emit(e, h0, h1):
+                if e == "S":
+                    nc.scalar.activation(out=o[:, h0:h1, jj, :], in_=src[:, h0:h1, :], func=IDENT, bias=bcol)
+                else:
+                    nc.vector.tensor_scalar(out=o[:, h0:h1, jj, :], in0=src[:, h0:h1, :], scalar1=bcol, scalar2=None, op0=ADD)
+
+            r0 = c * N + q * 512
+
+            def store(eng, h0, h1, j0, j1):
+                dst = out[b, h0:h1, r0:r0 + 512, :].rearrange("h (p j) d -> p h j d", j=4)[:, :, j0:j1, :]
+                eng.dma_start(out=dst.rearrange("p h j d -> p h (j d)"),
+                              in_=o[:, h0:h1, j0:j1, :].rearrange("p h j d -> p h (j d)"))
+
+            if last:
+                emit("V", 0, 2)
+                emit("S", 2, 4)
+                store(nc.sync, 0, 2, 2, 4)
+                store(nc.scalar, 2, 4, 2, 4)
+            else:
+                emit(evac_engine("o"), 0, NH)
+                if pair == 3 or (pair == 2 and q == 1):
+                    if jj % 2 == 1:
+                        store(nc.sync, 0, NH, jj - 1, jj + 1)
+                elif jj == 3:
+                    store(nc.sync, 0, NH, 0, 4)
+
+        schedule = build_schedule()
+        for n, job in enumerate(schedule):
+            for ahead in schedule[n:n + LEAD + 1]:
+                deinterleave(ahead)
+            kind = job[0]
+            if kind == "W":
+                do_w(job[1])
+            elif kind == "X":
+                do_x(job[1], job[2])
+            elif kind == "P":
+                do_p(job[1], job[2])
+            elif kind == "S":
+                do_s(job[1], job[2])
+            else:
+                do_o(job[1], job[2])
+            count[0] += 1
+            ready = [d for d in due if d[0] <= count[0]]
+            for d in ready:
+                due.remove(d)
+                d[1]()

@@ -18,39 +18,11 @@ ADD = mybir.AluOpType.add
 MULT = mybir.AluOpType.mult
 IDENT = mybir.ActivationFunctionType.Identity
 P = 128
-
-EVAC = {"t": "SVS", "s": "SSSV", "o": "SSVSSSV"}
-QDELAY = 3
-LEAD = 10
-DEINT_X = [6,7]
-DEINT_P = [8,9,10,11,12,13,14,15]
-DEINT_ENGINE = "V"
-
-
-def build_schedule():
-    def xj(i):
-        return [("X", i, 0), ("X", i, 1)]
-
-    def pj(c, js):
-        return [("P", c, j) for j in js]
-
-    def sj(i, hs=(0, 1, 2, 3)):
-        return [("S", i, h) for h in hs]
-
-    def oj(pair, js):
-        return [("O", pair, j) for j in js]
-
-    w = [("W", 0, 0), ("W", 1, 0)]
-    return (
-        xj(0) + w + pj(0, [0, 1]) + pj(0, [2, 3]) + pj(0, [4, 5]) + xj(1)
-        + pj(0, [6, 7]) + xj(2) + xj(3) + sj(0) + xj(4) + sj(1)
-        + sj(2) + xj(5) + oj(0, [0, 1]) + sj(3) + oj(0, [2, 3]) + sj(4)
-        + pj(1, [0, 1]) + oj(0, [4, 5]) + oj(0, [6, 7]) + sj(5, [0, 1]) + oj(1, [0, 1]) + xj(6)
-        + xj(7) + oj(1, [2, 3]) + sj(5, [2, 3]) + oj(1, [4, 5]) + pj(1, [2, 3]) + pj(1, [4, 5])
-        + sj(6, [0, 1]) + oj(1, [6, 7]) + oj(2, [0, 1]) + oj(2, [2, 3]) + sj(6, [2, 3]) + pj(1, [6, 7])
-        + sj(7) + oj(2, [4, 5]) + oj(2, [6, 7]) + oj(3, [0, 1]) + oj(3, [2, 3]) + oj(3, [4, 5])
-        + oj(3, [6, 7])
-    )
+UNITS = 8
+ROWS = 8
+FIRST_SORTED_STEP = 2
+TAIL_HEADS = 1
+SCALAR_OUT_EVERY = 8
 
 
 def tile_causalselfattention_pa_t_kernel(tc, x, wk_bytes, wk_scale, pk_w, pk_b, out):
@@ -66,54 +38,40 @@ def tile_causalselfattention_pa_t_kernel(tc, x, wk_bytes, wk_scale, pk_w, pk_b, 
         ws = keep.tile([P, 4], F32, name="ws", align_bytes=64)
         nc.scalar.dma_start(out=ws[:], in_=wk_scale.rearrange("o (p t) -> p (o t)", t=4))
 
-        xraw = {}
-        praw = {}
+        xraw, praw = {}, {}
 
-        def load_x(i, pieces):
+        def load_x(i):
             pair, u = divmod(i, 2)
             c, b = divmod(pair, 2)
             r0 = c * N + u * 512
-            t = keep.tile([P, 4, C], BF16, name="xraw%d" % i, align_bytes=64)
-            src = x[b, r0:r0 + 512, :].rearrange("(m t) k -> m t k", t=4)
-            n = 4 // pieces
+            src = x[b, r0:r0 + 512, :].rearrange("(m t) k -> m (t k)", t=4)
+            pieces = 2 if i == 0 else 1
+            w = 4 * C // pieces
+            parts = []
             for s in range(pieces):
-                nc.sync.dma_start(out=t[:, s * n:(s + 1) * n, :], in_=src[:, s * n:(s + 1) * n, :])
-            xraw[i] = t
+                t = keep.tile([P, w], BF16, name="xraw%d_%d" % (i, s), align_bytes=64)
+                nc.sync.dma_start(out=t[:], in_=src[:, s * w:(s + 1) * w])
+                parts.append(t)
+            xraw[i] = [parts[a * pieces // 2][:, (a * 1024) % w:(a * 1024) % w + 1024].bitcast(F32) for a in range(2)]
 
-        def load_p(c, q, half):
-            if (c, q) not in praw:
-                praw[(c, q)] = keep.tile([P, 4, N], BF16, name="praw%d%d" % (c, q), align_bytes=64)
-            src = pk_w[c, q * 512:(q + 1) * 512, :].rearrange("(m j) k -> m j k", j=4)
-            rows = slice(2 * half, 2 * half + 2)
-            nc.sync.dma_start(out=praw[(c, q)][:, rows, :], in_=src[:, rows, :])
+        def load_p(g):
+            c, q = divmod(g, 4)
+            t = keep.tile([P, 2 * N], BF16, name="praw%d" % g, align_bytes=64)
+            src = pk_w[c].rearrange("(m j) k -> m (j k)", j=ROWS)
+            nc.sync.dma_start(out=t[:], in_=src[:, 2 * q * N:2 * (q + 1) * N])
+            praw[g] = [t[:, a * N:(a + 1) * N].bitcast(F32) for a in range(2)]
 
-        load_x(0, 2)
-        bias_bf = keep.tile([P, 4, 4], BF16, name="bias_bf", align_bytes=64)
-        bias = keep.tile([P, 16], F32, name="bias", align_bytes=64)
-        load_p(0, 0, 0)
-        load_p(0, 0, 1)
-        load_p(0, 1, 0)
-        load_x(1, 1)
-        load_p(0, 1, 1)
-        load_x(2, 1)
-        load_x(3, 1)
-        load_x(4, 1)
-        load_x(5, 1)
-        load_p(1, 0, 0)
-        load_x(6, 1)
-        nc.sync.dma_start(out=bias_bf[:], in_=pk_b.rearrange("c (q p j) -> p (c q) j", q=2, j=4))
-        load_x(7, 1)
-        load_p(1, 0, 1)
-        load_p(1, 1, 0)
-        load_p(1, 1, 1)
+        bias = keep.tile([P, NC, ROWS], BF16, name="bias", align_bytes=64)
+        load_x(0)
+        for k in range(UNITS):
+            if k + 1 < UNITS:
+                load_x(k + 1)
+            load_p(k)
+            if k == 1:
+                nc.sync.dma_start(out=bias[:], in_=pk_b.rearrange("c (p j) -> p c j", j=ROWS))
 
-        warm = keep.tile([P, 1], F32, name="warm")
-        warm2 = keep.tile([P, 1], F32, name="warm2")
-        nc.vector.memset(warm[:], 0.0)
-        nc.scalar.activation(out=warm2[:], in_=warm[:], func=IDENT)
         ident = keep.tile([P, P], F32, name="ident", align_bytes=64)
         make_identity(nc, ident[:])
-        nc.gpsimd.tensor_copy(out=bias[:], in_=bias_bf[:].rearrange("p a j -> p (a j)"))
 
         wv = keep.tile([P, 4, C], BF16, name="wv", align_bytes=64)
         nc.vector.tensor_copy(out=wv[:, 0:2, :].rearrange("p i k -> p (i k)"),
@@ -125,61 +83,51 @@ def tile_causalselfattention_pa_t_kernel(tc, x, wk_bytes, wk_scale, pk_w, pk_b, 
         wcodes = keep.tile([P, C], U32, name="wcodes", align_bytes=64)
         wscales = keep.tile([P, C], U8, name="wscales", align_bytes=64)
 
-        xcodes, xscales, pcodes, pscales, kcodes, kscales, otiles = {}, {}, {}, {}, {}, {}, {}
-        grouped = {}
-        due = []
-        count = [0, 0]
-        evac_count = {}
-        words = {}
+        grouped, codes, scales, words, otiles = {}, {}, {}, {}, {}
 
-        def evac_engine(kind):
-            n = evac_count.get(kind, 0)
-            evac_count[kind] = n + 1
-            return EVAC[kind][n % len(EVAC[kind])]
-
-        def copy_out(kind, out_, in_):
-            if evac_engine(kind) == "S":
-                nc.scalar.copy(out=out_, in_=in_)
+        def copy_out(on_vector, dst, src):
+            if on_vector:
+                nc.vector.tensor_copy(out=dst, in_=src)
             else:
-                nc.vector.tensor_copy(out=out_, in_=in_)
+                nc.scalar.copy(out=dst, in_=src)
 
-        def later(fn, delay=QDELAY):
-            due.append((count[0] + delay, fn))
+        def raw(key, a):
+            return xraw[key[1]][a] if key[0] == "X" else praw[key[1]][a]
 
-        def quant(codes, scales, src):
-            nc.vector.quantize_mx(out=codes[:].bitcast(FP8X4), scales=scales[:], in_=src[:])
+        def sort(key):
+            d = work.tile([P, 2, 4, P], F32, name="sorted", bufs=4, align_bytes=64)
+            for a in range(2):
+                nc.vector.tensor_copy(out=d[:, a].rearrange("p (g u) m -> p g u m", g=2),
+                                      in_=raw(key, a).rearrange("p (g m u) -> p g u m", g=2, u=2))
+                words[key, a] = [d[:, a, n, :] for n in range(4)]
 
-        def raw_words(kind, i, a):
-            if kind == "X":
-                return xraw[i][:, 2 * a:2 * a + 2, :].rearrange("p s k -> p (s k)").bitcast(F32)
-            return praw[(i, a // 4)][:, a % 4, :].bitcast(F32)
-
-        def deinterleave(job):
-            kind = job[0]
-            if job in words:
-                return
-            if (kind == "X" and job[1] in DEINT_X) or (kind == "P" and (job[1] * 8 + job[2]) in DEINT_P):
-                d = work.tile([P, 4, P], F32, name="deint", bufs=10, align_bytes=64)
-                eng = nc.vector if DEINT_ENGINE == "V" else nc.gpsimd
-                eng.tensor_copy(out=d[:].rearrange("p (g u) m -> p g u m", g=2),
-                                in_=raw_words(*job).rearrange("p (g m u) -> p g u m", g=2, u=2))
-                words[job] = [d[:, n, :] for n in range(4)]
-            elif kind in ("X", "P"):
-                r = raw_words(*job)
-                words[job] = [r[:, 256 * g + u:256 * (g + 1):2] for g in range(2) for u in range(2)]
-
-        def bank(name):
-            return psum.tile([P, 512], F32, name="bank")
-
-        def turn(job, dst):
-            bk = bank("t")
+        def turn(key, a, on_vector=False):
+            if a == 0:
+                grouped[key] = work.tile([P, 2048], BF16, name="grouped", bufs=6, align_bytes=64)
+            r = raw(key, a)
+            src = words.get((key, a), [r[:, 256 * g + u:256 * (g + 1):2] for g in range(2) for u in range(2)])
+            bk = psum.tile([P, 512], F32, name="bank")
             for n in range(4):
-                nc.tensor.transpose(bk[:, n * P:(n + 1) * P], words[job][n], ident[:])
-            copy_out("t", dst.bitcast(F32).rearrange("p (g m u) -> p g m u", g=2, u=2),
+                nc.tensor.transpose(bk[:, n * P:(n + 1) * P], src[n], ident[:])
+            copy_out(on_vector,
+                     grouped[key][:, a * 1024:(a + 1) * 1024].bitcast(F32).rearrange("p (g m u) -> p g m u", g=2, u=2),
                      bk[:].rearrange("p (g u m) -> p g m u", g=2, u=2))
 
-        def do_w(a):
-            bk = bank("w")
+        def quantise(key):
+            codes[key] = keep.tile([P, 512], U32, name="codes%s%d" % key, align_bytes=64)
+            scales[key] = keep.tile([P, 512], U8, name="scales%s%d" % key, align_bytes=64)
+            nc.vector.quantize_mx(out=codes[key][:].bitcast(FP8X4), scales=scales[key][:], in_=grouped[key][:])
+
+        def quantise_half(key, a):
+            if a == 0:
+                codes[key] = keep.tile([P, 512], U32, name="codes%s%d" % key, align_bytes=64)
+                scales[key] = keep.tile([P, 512], U8, name="scales%s%d" % key, align_bytes=64)
+            nc.vector.quantize_mx(out=codes[key][:, a * 256:(a + 1) * 256].bitcast(FP8X4),
+                                  scales=scales[key][:, a * 256:(a + 1) * 256],
+                                  in_=grouped[key][:, a * 1024:(a + 1) * 1024])
+
+        def turn_w(a):
+            bk = psum.tile([P, 512], F32, name="bank")
             for i2 in range(2):
                 ww = wv[:, 2 * a + i2, :].bitcast(F32)
                 for u in range(2):
@@ -193,117 +141,129 @@ def tile_causalselfattention_pa_t_kernel(tc, x, wk_bytes, wk_scale, pk_w, pk_b, 
                     in0=vals[:, i2 * 512:(i2 + 1) * 512].rearrange("p (u r e) -> p r u e", u=2, e=2),
                     in1=ws[:].rearrange("p (u e) -> p u e", u=2).unsqueeze(1).to_broadcast([P, P, 2, 2]),
                     op=MULT)
-            later(lambda: nc.vector.quantize_mx(
-                out=wcodes[:, a * 256:(a + 1) * 256].bitcast(FP8X4),
-                scales=wscales[:, a * 256:(a + 1) * 256],
-                in_=wg[:, a * 1024:(a + 1) * 1024]), 1)
 
-        def do_x(i, a):
-            if a == 0:
-                grouped[("X", i)] = work.tile([P, 2048], BF16, name="xg", align_bytes=64)
-            g = grouped[("X", i)]
-            turn(("X", i, a), g[:, a * 1024:(a + 1) * 1024])
-            if a == 1:
-                xcodes[i] = work.tile([P, C], U32, name="xcodes", bufs=6, align_bytes=64)
-                xscales[i] = work.tile([P, C], U8, name="xscales", bufs=6, align_bytes=64)
-                later(lambda: quant(xcodes[i], xscales[i], g))
+        def quantise_w(a):
+            nc.vector.quantize_mx(out=wcodes[:, a * 256:(a + 1) * 256].bitcast(FP8X4),
+                                  scales=wscales[:, a * 256:(a + 1) * 256], in_=wg[:, a * 1024:(a + 1) * 1024])
 
-        def do_p(c, j):
-            key = (c, j // 2)
-            if j % 2 == 0:
-                grouped[("P",) + key] = work.tile([P, 2048], BF16, name="pg", align_bytes=64)
-            g = grouped[("P",) + key]
-            turn(("P", c, j), g[:, (j % 2) * 1024:(j % 2 + 1) * 1024])
-            if j % 2 == 1:
-                pcodes[key] = keep.tile([P, 512], U32, name="pcodes%d%d" % key, align_bytes=64)
-                pscales[key] = keep.tile([P, 512], U8, name="pscales%d%d" % key, align_bytes=64)
-                later(lambda: quant(pcodes[key], pscales[key], g))
-
-        def do_s(i, h):
+        def project(i, h, on_vector=False):
+            key = ("K", i)
             if h == 0:
-                grouped[("K", i)] = work.tile([P, 2048], BF16, name="kg", align_bytes=64)
-            g = grouped[("K", i)]
-            bk = bank("s")
+                grouped[key] = work.tile([P, 2048], BF16, name="grouped", bufs=6, align_bytes=64)
+            bk = psum.tile([P, 512], F32, name="bank")
             for t in range(4):
                 nc.tensor.matmul_mx(
                     out=bk[:, t * P:(t + 1) * P],
-                    lhsT=xcodes[i][:, t * P:(t + 1) * P].bitcast(FP8X4),
-                    lhsT_scale=xscales[i][:, t * P:(t + 1) * P],
+                    lhsT=codes["X", i][:, t * P:(t + 1) * P].bitcast(FP8X4),
+                    lhsT_scale=scales["X", i][:, t * P:(t + 1) * P],
                     rhs=wcodes[:, h * P:(h + 1) * P].bitcast(FP8X4),
                     rhs_scale=wscales[:, h * P:(h + 1) * P],
                     start=True, stop=True)
-            copy_out("s", g[:, h * 512:(h + 1) * 512].rearrange("p (n t) -> p n t", t=4),
+            copy_out(on_vector, grouped[key][:, h * 512:(h + 1) * 512].rearrange("p (n t) -> p n t", t=4),
                      bk[:].rearrange("p (t n) -> p n t", t=4))
-            if h == 3:
-                kcodes[i] = work.tile([P, C], U32, name="kcodes", bufs=8, align_bytes=64)
-                kscales[i] = work.tile([P, C], U8, name="kscales", bufs=8, align_bytes=64)
-                later(lambda: quant(kcodes[i], kscales[i], g))
 
-        def do_o(pair, j):
+        def mix(pair, j, on_vector):
             c, b = divmod(pair, 2)
-            q, jj = divmod(j, 4)
-            if jj == 0:
-                otiles[(pair, q)] = work.tile([P, NH, 4, D], F32, name="o", align_bytes=64)
-            o = otiles[(pair, q)]
-            bk = bank("o")
-            s0 = (j % 2) * 256
-            key = (c, j // 2)
+            if j == 0:
+                otiles[pair] = work.tile([P, NH, ROWS, D], F32, name="o", bufs=3, align_bytes=64)
+            o = otiles[pair]
+            key = ("P", 4 * c + j // 2)
+            bk = psum.tile([P, 512], F32, name="bank")
             for u in range(2):
-                cols = slice(s0 + u * P, s0 + (u + 1) * P)
+                cols = slice((j % 2) * 256 + u * P, (j % 2) * 256 + (u + 1) * P)
                 nc.tensor.matmul_mx(
                     out=bk[:],
-                    lhsT=pcodes[key][:, cols].bitcast(FP8X4),
-                    lhsT_scale=pscales[key][:, cols],
-                    rhs=kcodes[2 * pair + u][:].bitcast(FP8X4),
-                    rhs_scale=kscales[2 * pair + u][:],
+                    lhsT=codes[key][:, cols].bitcast(FP8X4), lhsT_scale=scales[key][:, cols],
+                    rhs=codes["K", 2 * pair + u][:].bitcast(FP8X4), rhs_scale=scales["K", 2 * pair + u][:],
                     start=(u == 0), stop=(u == 1))
-            bcol = bias[:, (2 * c + q) * 4 + jj:(2 * c + q) * 4 + jj + 1]
             src = bk[:].rearrange("p (h d) -> p h d", h=NH)
-            last = pair == 3 and j == 7
-
-            def emit(e, h0, h1):
-                if e == "S":
-                    nc.scalar.activation(out=o[:, h0:h1, jj, :], in_=src[:, h0:h1, :], func=IDENT, bias=bcol)
-                else:
-                    nc.vector.tensor_scalar(out=o[:, h0:h1, jj, :], in0=src[:, h0:h1, :], scalar1=bcol, scalar2=None, op0=ADD)
-
-            r0 = c * N + q * 512
-
-            def store(eng, h0, h1, j0, j1):
-                dst = out[b, h0:h1, r0:r0 + 512, :].rearrange("h (p j) d -> p h j d", j=4)[:, :, j0:j1, :]
-                eng.dma_start(out=dst.rearrange("p h j d -> p h (j d)"),
-                              in_=o[:, h0:h1, j0:j1, :].rearrange("p h j d -> p h (j d)"))
-
-            if last:
-                emit("V", 0, 2)
-                emit("S", 2, 4)
-                store(nc.sync, 0, 2, 2, 4)
-                store(nc.scalar, 2, 4, 2, 4)
+            if on_vector:
+                nc.vector.tensor_scalar(out=o[:, :, j, :], in0=src, scalar1=bias[:, c, j:j + 1], scalar2=None, op0=ADD)
             else:
-                emit(evac_engine("o"), 0, NH)
-                if pair == 3 or (pair == 2 and q == 1):
-                    if jj % 2 == 1:
-                        store(nc.sync, 0, NH, jj - 1, jj + 1)
-                elif jj == 3:
-                    store(nc.sync, 0, NH, 0, 4)
+                nc.scalar.activation(out=o[:, :, j, :], in_=src, func=IDENT, bias=bias[:, c, j:j + 1])
 
-        schedule = build_schedule()
-        for n, job in enumerate(schedule):
-            for ahead in schedule[n:n + LEAD + 1]:
-                deinterleave(ahead)
-            kind = job[0]
-            if kind == "W":
-                do_w(job[1])
-            elif kind == "X":
-                do_x(job[1], job[2])
-            elif kind == "P":
-                do_p(job[1], job[2])
-            elif kind == "S":
-                do_s(job[1], job[2])
+        def mix_narrow(pair, h0, j0, on_vector):
+            c, b = divmod(pair, 2)
+            if (h0, j0) == (0, 0):
+                otiles[pair] = work.tile([P, NH, ROWS, D], F32, name="o", bufs=3, align_bytes=64)
+            o = otiles[pair]
+            nj = NH // TAIL_HEADS
+            w = TAIL_HEADS * D
+            bk = psum.tile([P, 512], F32, name="bank")
+            for jj in range(nj):
+                j = j0 + jj
+                key = ("P", 4 * c + j // 2)
+                for u in range(2):
+                    cols = slice((j % 2) * 256 + u * P, (j % 2) * 256 + (u + 1) * P)
+                    nc.tensor.matmul_mx(
+                        out=bk[:, jj * w:(jj + 1) * w],
+                        lhsT=codes[key][:, cols].bitcast(FP8X4), lhsT_scale=scales[key][:, cols],
+                        rhs=codes["K", 2 * pair + u][:, h0 * D:h0 * D + w].bitcast(FP8X4),
+                        rhs_scale=scales["K", 2 * pair + u][:, h0 * D:h0 * D + w],
+                        start=(u == 0), stop=(u == 1))
+            src = bk[:].rearrange("p (j h d) -> p j h d", j=nj, d=D)
+            dst = o[:, h0:h0 + TAIL_HEADS, j0:j0 + nj, :].rearrange("p h j d -> p j h d")
+            if on_vector:
+                nc.vector.tensor_tensor(out=dst, in0=src, op=ADD,
+                                        in1=bias[:, c, j0:j0 + nj].unsqueeze(2).unsqueeze(3).to_broadcast([P, nj, TAIL_HEADS, D]))
             else:
-                do_o(job[1], job[2])
-            count[0] += 1
-            ready = [d for d in due if d[0] <= count[0]]
-            for d in ready:
-                due.remove(d)
-                d[1]()
+                for jj in range(nj):
+                    nc.scalar.activation(out=dst[:, jj], in_=src[:, jj], func=IDENT, bias=bias[:, c, j0 + jj:j0 + jj + 1])
+
+        def store(pair, j0, j1, h0=0, h1=NH):
+            c, b = divmod(pair, 2)
+            dst = out[b, :, c * N:(c + 1) * N, :].rearrange("h (p j) d -> p h (j d)", j=ROWS)
+            nc.sync.dma_start(out=dst[:, h0:h1, j0 * D:j1 * D],
+                              in_=otiles[pair][:].rearrange("p h j d -> p h (j d)")[:, h0:h1, j0 * D:j1 * D])
+
+        turn_w(0)
+        turn(("X", 0), 0)
+        turn_w(1)
+        turn(("X", 0), 1)
+        quantise_w(0)
+        quantise(("X", 0))
+        quantise_w(1)
+
+        for k in range(UNITS):
+            turned = [key for key in (("P", k), ("X", k + 1)) if key[1] < UNITS]
+            to_sort = [key for key in (("P", k + 1), ("X", k + 2)) if key[1] < UNITS and k + 1 >= FIRST_SORTED_STEP]
+            mixing = k >= 2
+            last = k == UNITS - 1
+            pair, half = divmod(k - 2, 2)
+            if k == 0:
+                turned.reverse()
+            for n, key in enumerate(turned):
+                turn(key, 0)
+                turn(key, 1, on_vector=not mixing and n == 1 and False)
+            if k >= 1:
+                quantise(("K", k - 1))
+            for key in to_sort[:1]:
+                sort(key)
+            for key in turned[:1]:
+                quantise(key)
+            for key in to_sort[1:]:
+                sort(key)
+            heads = [[0, 1], [2, 3], [], []] if last else [[0, 1], [2], [3], []]
+            for n in range(4):
+                for h in heads[n]:
+                    project(k, h, on_vector=not mixing and h in (3,))
+                if mixing:
+                    j = 4 * half + n
+                    mix(pair, j, on_vector=(j % SCALAR_OUT_EVERY != SCALAR_OUT_EVERY - 1))
+                if n == 0:
+                    for key in turned[1:]:
+                        quantise(key)
+                if last and n in (1, 2):
+                    quantise_half(("K", k), n - 1)
+                if k >= 7 and n % 2 == 1:
+                    store(pair, 4 * half + n - 1, 4 * half + n + 1)
+            if mixing and k < 7:
+                store(pair, 4 * half, 4 * half + 4)
+        nj = NH // TAIL_HEADS
+        n = 0
+        for h0 in range(0, NH, TAIL_HEADS):
+            for j0 in range(0, ROWS, nj):
+                mix_narrow(3, h0, j0, on_vector=n % 2 == 0)
+                n += 1
+                if (j0 + nj) % 4 == 0:
+                    store(3, j0 + nj - 4, j0 + nj, h0, h0 + TAIL_HEADS)

@@ -17,73 +17,106 @@ FP8X4 = mybir.dt.float8_e4m3fn_x4
 ADD = mybir.AluOpType.add
 MULT = mybir.AluOpType.mult
 IDENT = mybir.ActivationFunctionType.Identity
+
 P = 128
-UNITS = 8
-ROWS = 8
-FIRST_SORTED_STEP = 2
-TAIL_HEADS = 1
-SCALAR_OUT_EVERY = 8
+BANKS = 8
+ROWS = N // P
+PAIRS = B * NC
+VECTOR_EVERY = 4
+VECTOR_FROM = 11
+TURN_DELAY = 2
+PROJECT_DELAY = 1
+SORT_LEAD = 9
+UNSORTED = 6
+
+
+def tensor_jobs():
+    def turn(*keys):
+        return [("turn", key, a) for key in keys for a in range(2)]
+
+    def project(unit, heads):
+        return [("project", unit, h) for h in heads]
+
+    jobs = [("turn_w", a) for a in range(2)] + turn(("X", 0), ("X", 1), ("P", 0))
+    jobs += project(0, range(NH)) + project(1, range(NH))
+    turns = [[("P", 1), ("X", 2), ("X", 3), ("P", 2), ("P", 3)],
+             [("X", 4), ("X", 5), ("P", 4), ("P", 5)],
+             [("X", 6), ("X", 7), ("P", 6), ("P", 7)]]
+    for pair in range(PAIRS - 2):
+        jobs += turn(*turns[pair])
+        mixes = [("mix", pair, j) for j in range(ROWS)]
+        projections = project(2 * pair + 2, range(NH)) + project(2 * pair + 3, range(NH))
+        jobs += mixes[:2]
+        for n in range(4):
+            jobs += projections[2 * n:2 * n + 2] + [mixes[2 + n]]
+        jobs += mixes[6:]
+    jobs += turn(*turns[2])
+    mixes = [("mix", 2, j) for j in range(ROWS)]
+    mixes += [("mix_half", 3, h0, j0) for h0 in (0, 2) for j0 in range(0, ROWS, 2)]
+    projections = [job for h0 in (0, 2) for unit in (6, 7) for job in project(unit, (h0, h0 + 1))]
+    jobs += mixes[:2]
+    for n, job in enumerate(projections):
+        jobs += [job, mixes[2 + n]]
+    jobs += mixes[2 + len(projections):]
+    return jobs
 
 
 def tile_causalselfattention_pa_t_kernel(tc, x, wk_bytes, wk_scale, pk_w, pk_b, out):
     nc = tc.nc
+    jobs = tensor_jobs()
+    turn_jobs = [job for job in jobs if job[0] == "turn"]
     with ExitStack() as ctx:
         keep = ctx.enter_context(tc.tile_pool(name="keep", bufs=1))
-        work = ctx.enter_context(tc.tile_pool(name="work", bufs=3))
-        psum = ctx.enter_context(tc.psum_pool(name="psum", bufs=8))
+        work = ctx.enter_context(tc.tile_pool(name="work", bufs=1))
+        psum = ctx.enter_context(tc.psum_pool(name="psum", bufs=BANKS))
         ctx.enter_context(tc.manual_schedule())
 
-        wb = keep.tile([P, 4, C], U8, name="wb", align_bytes=64)
-        nc.sync.dma_start(out=wb[:], in_=wk_bytes.rearrange("(i r) k -> r i k", r=P))
+        wb = []
+        for a in range(2):
+            t = keep.tile([P, 2, C], U8, name="wb%d" % a, align_bytes=64)
+            nc.sync.dma_start(out=t[:], in_=wk_bytes.rearrange("(i r) k -> r i k", r=P)[:, 2 * a:2 * a + 2, :])
+            wb.append(t)
         ws = keep.tile([P, 4], F32, name="ws", align_bytes=64)
         nc.scalar.dma_start(out=ws[:], in_=wk_scale.rearrange("o (p t) -> p (o t)", t=4))
 
-        xraw, praw = {}, {}
+        raw = {}
 
-        def load_x(i):
-            pair, u = divmod(i, 2)
-            c, b = divmod(pair, 2)
-            r0 = c * N + u * 512
-            src = x[b, r0:r0 + 512, :].rearrange("(m t) k -> m (t k)", t=4)
-            pieces = 2 if i == 0 else 1
-            w = 4 * C // pieces
-            parts = []
+        def load(key, pieces):
+            kind, i = key
+            if kind == "X":
+                c, b, u = i // 4, i // 2 % 2, i % 2
+                r0 = c * N + u * 512
+                src = x[b, r0:r0 + 512, :].rearrange("(m t) k -> m (t k)", t=4)
+            else:
+                c, q = divmod(i, 4)
+                src = pk_w[c].rearrange("(m j) k -> m (j k)", j=ROWS)[:, 2 * q * N:2 * (q + 1) * N]
+            w = 2048 // pieces
             for s in range(pieces):
-                t = keep.tile([P, w], BF16, name="xraw%d_%d" % (i, s), align_bytes=64)
+                t = keep.tile([P, w], BF16, name="raw%s%d_%d" % (kind, i, s), align_bytes=64)
                 nc.sync.dma_start(out=t[:], in_=src[:, s * w:(s + 1) * w])
-                parts.append(t)
-            xraw[i] = [parts[a * pieces // 2][:, (a * 1024) % w:(a * 1024) % w + 1024].bitcast(F32) for a in range(2)]
-
-        def load_p(g):
-            c, q = divmod(g, 4)
-            t = keep.tile([P, 2 * N], BF16, name="praw%d" % g, align_bytes=64)
-            src = pk_w[c].rearrange("(m j) k -> m (j k)", j=ROWS)
-            nc.sync.dma_start(out=t[:], in_=src[:, 2 * q * N:2 * (q + 1) * N])
-            praw[g] = [t[:, a * N:(a + 1) * N].bitcast(F32) for a in range(2)]
+                for a in range(2 // pieces):
+                    raw[key, s + a] = t[:, a * 1024:(a + 1) * 1024].bitcast(F32)
 
         bias = keep.tile([P, NC, ROWS], BF16, name="bias", align_bytes=64)
-        load_x(0)
-        for k in range(UNITS):
-            if k + 1 < UNITS:
-                load_x(k + 1)
-            load_p(k)
-            if k == 1:
+        for n, job in enumerate(turn_jobs[::2]):
+            load(job[1], 2 if n == 0 else 1)
+            if n == 3:
                 nc.sync.dma_start(out=bias[:], in_=pk_b.rearrange("c (p j) -> p c j", j=ROWS))
 
         ident = keep.tile([P, P], F32, name="ident", align_bytes=64)
         make_identity(nc, ident[:])
 
         wv = keep.tile([P, 4, C], BF16, name="wv", align_bytes=64)
-        nc.vector.tensor_copy(out=wv[:, 0:2, :].rearrange("p i k -> p (i k)"),
-                              in_=wb[:, 0:2, :].rearrange("p i k -> p (i k)").bitcast(FP8))
-        nc.scalar.copy(out=wv[:, 2:4, :].rearrange("p i k -> p (i k)"),
-                       in_=wb[:, 2:4, :].rearrange("p i k -> p (i k)").bitcast(FP8))
-
-        wg = keep.tile([P, C * 4], BF16, name="wg", align_bytes=64)
-        wcodes = keep.tile([P, C], U32, name="wcodes", align_bytes=64)
-        wscales = keep.tile([P, C], U8, name="wscales", align_bytes=64)
+        for a in range(2):
+            nc.vector.tensor_copy(out=wv[:, 2 * a:2 * a + 2, :].rearrange("p i k -> p (i k)"),
+                                  in_=wb[a][:].rearrange("p i k -> p (i k)").bitcast(FP8))
 
         grouped, codes, scales, words, otiles = {}, {}, {}, {}, {}
+
+        def new_operand(key):
+            grouped[key] = work.tile([P, 2048], BF16, name="grouped", bufs=6, align_bytes=64)
+            codes[key] = keep.tile([P, 512], U32, name="codes%s%d" % key, align_bytes=64)
+            scales[key] = keep.tile([P, 512], U8, name="scales%s%d" % key, align_bytes=64)
 
         def copy_out(on_vector, dst, src):
             if on_vector:
@@ -91,179 +124,141 @@ def tile_causalselfattention_pa_t_kernel(tc, x, wk_bytes, wk_scale, pk_w, pk_b, 
             else:
                 nc.scalar.copy(out=dst, in_=src)
 
-        def raw(key, a):
-            return xraw[key[1]][a] if key[0] == "X" else praw[key[1]][a]
+        def sort(key, a):
+            d = work.tile([P, 4, P], F32, name="sorted", bufs=10, align_bytes=64)
+            nc.vector.tensor_copy(out=d[:].rearrange("p (g u) m -> p g u m", g=2),
+                                  in_=raw[key, a].rearrange("p (g m u) -> p g u m", g=2, u=2))
+            words[key, a] = [d[:, n, :] for n in range(4)]
 
-        def sort(key):
-            d = work.tile([P, 2, 4, P], F32, name="sorted", bufs=4, align_bytes=64)
-            for a in range(2):
-                nc.vector.tensor_copy(out=d[:, a].rearrange("p (g u) m -> p g u m", g=2),
-                                      in_=raw(key, a).rearrange("p (g m u) -> p g u m", g=2, u=2))
-                words[key, a] = [d[:, a, n, :] for n in range(4)]
-
-        def turn(key, a, on_vector=False):
+        def turn(key, a, on_vector):
             if a == 0:
-                grouped[key] = work.tile([P, 2048], BF16, name="grouped", bufs=6, align_bytes=64)
-            r = raw(key, a)
+                new_operand(key)
+            r = raw[key, a]
             src = words.get((key, a), [r[:, 256 * g + u:256 * (g + 1):2] for g in range(2) for u in range(2)])
-            bk = psum.tile([P, 512], F32, name="bank")
+            bank = psum.tile([P, 512], F32, name="bank")
             for n in range(4):
-                nc.tensor.transpose(bk[:, n * P:(n + 1) * P], src[n], ident[:])
+                nc.tensor.transpose(bank[:, n * P:(n + 1) * P], src[n], ident[:])
             copy_out(on_vector,
                      grouped[key][:, a * 1024:(a + 1) * 1024].bitcast(F32).rearrange("p (g m u) -> p g m u", g=2, u=2),
-                     bk[:].rearrange("p (g u m) -> p g m u", g=2, u=2))
+                     bank[:].rearrange("p (g u m) -> p g m u", g=2, u=2))
 
-        def quantise(key):
-            codes[key] = keep.tile([P, 512], U32, name="codes%s%d" % key, align_bytes=64)
-            scales[key] = keep.tile([P, 512], U8, name="scales%s%d" % key, align_bytes=64)
-            nc.vector.quantize_mx(out=codes[key][:].bitcast(FP8X4), scales=scales[key][:], in_=grouped[key][:])
-
-        def quantise_half(key, a):
-            if a == 0:
-                codes[key] = keep.tile([P, 512], U32, name="codes%s%d" % key, align_bytes=64)
-                scales[key] = keep.tile([P, 512], U8, name="scales%s%d" % key, align_bytes=64)
-            nc.vector.quantize_mx(out=codes[key][:, a * 256:(a + 1) * 256].bitcast(FP8X4),
-                                  scales=scales[key][:, a * 256:(a + 1) * 256],
-                                  in_=grouped[key][:, a * 1024:(a + 1) * 1024])
+        def quantise(key, c0, c1):
+            nc.vector.quantize_mx(out=codes[key][:, c0:c1].bitcast(FP8X4), scales=scales[key][:, c0:c1],
+                                  in_=grouped[key][:, 4 * c0:4 * c1])
 
         def turn_w(a):
-            bk = psum.tile([P, 512], F32, name="bank")
-            for i2 in range(2):
-                ww = wv[:, 2 * a + i2, :].bitcast(F32)
+            key = ("W", 0)
+            if a == 0:
+                new_operand(key)
+            bank = psum.tile([P, 512], F32, name="bank")
+            for i in range(2):
+                ww = wv[:, 2 * a + i, :].bitcast(F32)
                 for u in range(2):
-                    n = 2 * i2 + u
-                    nc.tensor.transpose(bk[:, n * P:(n + 1) * P], ww[:, u:256:2], ident[:])
-            vals = bk[:].bitcast(BF16)
-            for i2 in range(2):
-                base = (2 * a + i2) * 512
+                    n = 2 * i + u
+                    nc.tensor.transpose(bank[:, n * P:(n + 1) * P], ww[:, u:256:2], ident[:])
+            vals = bank[:].bitcast(BF16)
+            for i in range(2):
+                base = (2 * a + i) * 512
                 nc.vector.tensor_tensor(
-                    out=wg[:, base:base + 512].rearrange("p (r u e) -> p r u e", u=2, e=2),
-                    in0=vals[:, i2 * 512:(i2 + 1) * 512].rearrange("p (u r e) -> p r u e", u=2, e=2),
+                    out=grouped[key][:, base:base + 512].rearrange("p (r u e) -> p r u e", u=2, e=2),
+                    in0=vals[:, i * 512:(i + 1) * 512].rearrange("p (u r e) -> p r u e", u=2, e=2),
                     in1=ws[:].rearrange("p (u e) -> p u e", u=2).unsqueeze(1).to_broadcast([P, P, 2, 2]),
                     op=MULT)
 
-        def quantise_w(a):
-            nc.vector.quantize_mx(out=wcodes[:, a * 256:(a + 1) * 256].bitcast(FP8X4),
-                                  scales=wscales[:, a * 256:(a + 1) * 256], in_=wg[:, a * 1024:(a + 1) * 1024])
+        def mx_pass(dst, stationary, s0, moving, m0, width, start, stop):
+            nc.tensor.matmul_mx(
+                out=dst,
+                lhsT=codes[stationary][:, s0:s0 + P].bitcast(FP8X4), lhsT_scale=scales[stationary][:, s0:s0 + P],
+                rhs=codes[moving][:, m0:m0 + width].bitcast(FP8X4), rhs_scale=scales[moving][:, m0:m0 + width],
+                start=start, stop=stop)
 
-        def project(i, h, on_vector=False):
-            key = ("K", i)
+        def project(unit, h, on_vector):
+            key = ("K", unit)
             if h == 0:
-                grouped[key] = work.tile([P, 2048], BF16, name="grouped", bufs=6, align_bytes=64)
-            bk = psum.tile([P, 512], F32, name="bank")
+                new_operand(key)
+            bank = psum.tile([P, 512], F32, name="bank")
             for t in range(4):
-                nc.tensor.matmul_mx(
-                    out=bk[:, t * P:(t + 1) * P],
-                    lhsT=codes["X", i][:, t * P:(t + 1) * P].bitcast(FP8X4),
-                    lhsT_scale=scales["X", i][:, t * P:(t + 1) * P],
-                    rhs=wcodes[:, h * P:(h + 1) * P].bitcast(FP8X4),
-                    rhs_scale=wscales[:, h * P:(h + 1) * P],
-                    start=True, stop=True)
+                mx_pass(bank[:, t * P:(t + 1) * P], ("X", unit), t * P, ("W", 0), h * D, D, True, True)
             copy_out(on_vector, grouped[key][:, h * 512:(h + 1) * 512].rearrange("p (n t) -> p n t", t=4),
-                     bk[:].rearrange("p (t n) -> p n t", t=4))
+                     bank[:].rearrange("p (t n) -> p n t", t=4))
+
+        def out_tile(pair):
+            if pair not in otiles:
+                otiles[pair] = work.tile([P, NH, ROWS, D], F32, name="o", bufs=2, align_bytes=64)
+            return otiles[pair]
+
+        def mix_passes(dst, pair, j, h0, heads):
+            for u in range(2):
+                mx_pass(dst, ("P", 4 * (pair // 2) + j // 2), (j % 2) * 256 + u * P,
+                        ("K", 2 * pair + u), h0 * D, heads * D, u == 0, u == 1)
 
         def mix(pair, j, on_vector):
-            c, b = divmod(pair, 2)
-            if j == 0:
-                otiles[pair] = work.tile([P, NH, ROWS, D], F32, name="o", bufs=3, align_bytes=64)
-            o = otiles[pair]
-            key = ("P", 4 * c + j // 2)
-            bk = psum.tile([P, 512], F32, name="bank")
-            for u in range(2):
-                cols = slice((j % 2) * 256 + u * P, (j % 2) * 256 + (u + 1) * P)
-                nc.tensor.matmul_mx(
-                    out=bk[:],
-                    lhsT=codes[key][:, cols].bitcast(FP8X4), lhsT_scale=scales[key][:, cols],
-                    rhs=codes["K", 2 * pair + u][:].bitcast(FP8X4), rhs_scale=scales["K", 2 * pair + u][:],
-                    start=(u == 0), stop=(u == 1))
-            src = bk[:].rearrange("p (h d) -> p h d", h=NH)
+            bank = psum.tile([P, 512], F32, name="bank")
+            mix_passes(bank[:], pair, j, 0, NH)
+            src = bank[:].rearrange("p (h d) -> p h d", h=NH)
+            dst = out_tile(pair)[:, :, j, :]
+            column = bias[:, pair // 2, j:j + 1]
             if on_vector:
-                nc.vector.tensor_scalar(out=o[:, :, j, :], in0=src, scalar1=bias[:, c, j:j + 1], scalar2=None, op0=ADD)
+                nc.vector.tensor_scalar(out=dst, in0=src, scalar1=column, scalar2=None, op0=ADD)
             else:
-                nc.scalar.activation(out=o[:, :, j, :], in_=src, func=IDENT, bias=bias[:, c, j:j + 1])
+                nc.scalar.activation(out=dst, in_=src, func=IDENT, bias=column)
 
-        def mix_narrow(pair, h0, j0, on_vector):
-            c, b = divmod(pair, 2)
-            if (h0, j0) == (0, 0):
-                otiles[pair] = work.tile([P, NH, ROWS, D], F32, name="o", bufs=3, align_bytes=64)
-            o = otiles[pair]
-            nj = NH // TAIL_HEADS
-            w = TAIL_HEADS * D
-            bk = psum.tile([P, 512], F32, name="bank")
-            for jj in range(nj):
-                j = j0 + jj
-                key = ("P", 4 * c + j // 2)
-                for u in range(2):
-                    cols = slice((j % 2) * 256 + u * P, (j % 2) * 256 + (u + 1) * P)
-                    nc.tensor.matmul_mx(
-                        out=bk[:, jj * w:(jj + 1) * w],
-                        lhsT=codes[key][:, cols].bitcast(FP8X4), lhsT_scale=scales[key][:, cols],
-                        rhs=codes["K", 2 * pair + u][:, h0 * D:h0 * D + w].bitcast(FP8X4),
-                        rhs_scale=scales["K", 2 * pair + u][:, h0 * D:h0 * D + w],
-                        start=(u == 0), stop=(u == 1))
-            src = bk[:].rearrange("p (j h d) -> p j h d", j=nj, d=D)
-            dst = o[:, h0:h0 + TAIL_HEADS, j0:j0 + nj, :].rearrange("p h j d -> p j h d")
+        def mix_half(pair, h0, j0, on_vector):
+            bank = psum.tile([P, 512], F32, name="bank")
+            for jj in range(2):
+                mix_passes(bank[:, jj * 256:(jj + 1) * 256], pair, j0 + jj, h0, 2)
+            src = bank[:].rearrange("p (j h d) -> p j h d", j=2, d=D)
+            dst = out_tile(pair)[:, h0:h0 + 2, j0:j0 + 2, :].rearrange("p h j d -> p j h d")
+            columns = bias[:, pair // 2, j0:j0 + 2]
             if on_vector:
                 nc.vector.tensor_tensor(out=dst, in0=src, op=ADD,
-                                        in1=bias[:, c, j0:j0 + nj].unsqueeze(2).unsqueeze(3).to_broadcast([P, nj, TAIL_HEADS, D]))
+                                        in1=columns.unsqueeze(2).unsqueeze(3).to_broadcast([P, 2, 2, D]))
             else:
-                for jj in range(nj):
-                    nc.scalar.activation(out=dst[:, jj], in_=src[:, jj], func=IDENT, bias=bias[:, c, j0 + jj:j0 + jj + 1])
+                for jj in range(2):
+                    nc.scalar.activation(out=dst[:, jj], in_=src[:, jj], func=IDENT, bias=columns[:, jj:jj + 1])
 
-        def store(pair, j0, j1, h0=0, h1=NH):
+        def store(pair, h0, h1, j0, j1):
             c, b = divmod(pair, 2)
             dst = out[b, :, c * N:(c + 1) * N, :].rearrange("h (p j) d -> p h (j d)", j=ROWS)
-            nc.sync.dma_start(out=dst[:, h0:h1, j0 * D:j1 * D],
-                              in_=otiles[pair][:].rearrange("p h j d -> p h (j d)")[:, h0:h1, j0 * D:j1 * D])
+            src = otiles[pair][:].rearrange("p h j d -> p h (j d)")
+            nc.sync.dma_start(out=dst[:, h0:h1, j0 * D:j1 * D], in_=src[:, h0:h1, j0 * D:j1 * D])
 
-        turn_w(0)
-        turn(("X", 0), 0)
-        turn_w(1)
-        turn(("X", 0), 1)
-        quantise_w(0)
-        quantise(("X", 0))
-        quantise_w(1)
-
-        for k in range(UNITS):
-            turned = [key for key in (("P", k), ("X", k + 1)) if key[1] < UNITS]
-            to_sort = [key for key in (("P", k + 1), ("X", k + 2)) if key[1] < UNITS and k + 1 >= FIRST_SORTED_STEP]
-            mixing = k >= 2
-            last = k == UNITS - 1
-            pair, half = divmod(k - 2, 2)
-            if k == 0:
-                turned.reverse()
-            for n, key in enumerate(turned):
-                turn(key, 0)
-                turn(key, 1, on_vector=not mixing and n == 1 and False)
-            if k >= 1:
-                quantise(("K", k - 1))
-            for key in to_sort[:1]:
-                sort(key)
-            for key in turned[:1]:
-                quantise(key)
-            for key in to_sort[1:]:
-                sort(key)
-            heads = [[0, 1], [2, 3], [], []] if last else [[0, 1], [2], [3], []]
-            for n in range(4):
-                for h in heads[n]:
-                    project(k, h, on_vector=not mixing and h in (3,))
-                if mixing:
-                    j = 4 * half + n
-                    mix(pair, j, on_vector=(j % SCALAR_OUT_EVERY != SCALAR_OUT_EVERY - 1))
-                if n == 0:
-                    for key in turned[1:]:
-                        quantise(key)
-                if last and n in (1, 2):
-                    quantise_half(("K", k), n - 1)
-                if k >= 7 and n % 2 == 1:
-                    store(pair, 4 * half + n - 1, 4 * half + n + 1)
-            if mixing and k < 7:
-                store(pair, 4 * half, 4 * half + 4)
-        nj = NH // TAIL_HEADS
-        n = 0
-        for h0 in range(0, NH, TAIL_HEADS):
-            for j0 in range(0, ROWS, nj):
-                mix_narrow(3, h0, j0, on_vector=n % 2 == 0)
-                n += 1
-                if (j0 + nj) % 4 == 0:
-                    store(3, j0 + nj - 4, j0 + nj, h0, h0 + TAIL_HEADS)
+        to_sort = turn_jobs[UNSORTED:]
+        alternate_from = len(jobs) - 16
+        due = []
+        for n, job in enumerate(jobs):
+            if to_sort and to_sort[0] in jobs[n:n + SORT_LEAD + 1]:
+                sort(*to_sort.pop(0)[1:])
+            if n < alternate_from:
+                on_vector = n >= VECTOR_FROM and (n - VECTOR_FROM) % VECTOR_EVERY == 0
+            else:
+                on_vector = (n - alternate_from) % 2 == 0
+            kind = job[0]
+            if kind == "turn_w":
+                turn_w(job[1])
+                due.append((n + TURN_DELAY, ("W", 0), 256 * job[1], 256 * (job[1] + 1)))
+            elif kind == "turn":
+                turn(job[1], job[2], on_vector)
+                if job[2] == 1:
+                    due.append((n + TURN_DELAY, job[1], 0, 512))
+            elif kind == "project":
+                unit, h = job[1:]
+                project(unit, h, on_vector)
+                heads = 2 if unit // 2 == PAIRS - 1 else NH
+                if (h + 1) % heads == 0:
+                    due.append((n + PROJECT_DELAY, ("K", unit), (h + 1 - heads) * D, (h + 1) * D))
+            elif kind == "mix":
+                pair, j = job[1:]
+                mix(pair, j, on_vector)
+                rows = 2 if pair == PAIRS - 2 else 4
+                if (j + 1) % rows == 0:
+                    store(pair, 0, NH, j + 1 - rows, j + 1)
+            else:
+                pair, h0, j0 = job[1:]
+                mix_half(pair, h0, j0, on_vector)
+                rows = 2 if n >= len(jobs) - 2 else 4
+                if (j0 + 2) % rows == 0:
+                    store(pair, h0, h0 + 2, j0 + 2 - rows, j0 + 2)
+            for entry in [entry for entry in due if entry[0] <= n]:
+                due.remove(entry)
+                quantise(*entry[1:])

@@ -126,8 +126,8 @@ def tile_causalselfattention_pa_t_kernel(tc, x, wk_bytes, wk_scale, pk_w, pk_b, 
 
         def sort(key, a):
             d = work.tile([P, 4, P], F32, name="sorted", bufs=10, align_bytes=64)
-            nc.vector.tensor_copy(out=d[:].rearrange("p (g u) m -> p g u m", g=2),
-                                  in_=raw[key, a].rearrange("p (g m u) -> p g u m", g=2, u=2))
+            nc.vector.tensor_copy(out=d[:].rearrange("p (g u) (m i) -> p g m u i", g=2, i=4),
+                                  in_=raw[key, a].rearrange("p (g m i u) -> p g m u i", g=2, u=2, i=4))
             words[key, a] = [d[:, n, :] for n in range(4)]
 
         def turn(key, a, on_vector):
@@ -139,8 +139,8 @@ def tile_causalselfattention_pa_t_kernel(tc, x, wk_bytes, wk_scale, pk_w, pk_b, 
             for n in range(4):
                 nc.tensor.transpose(bank[:, n * P:(n + 1) * P], src[n], ident[:])
             copy_out(on_vector,
-                     grouped[key][:, a * 1024:(a + 1) * 1024].bitcast(F32).rearrange("p (g m u) -> p g m u", g=2, u=2),
-                     bank[:].rearrange("p (g u m) -> p g m u", g=2, u=2))
+                     grouped[key][:, a * 1024:(a + 1) * 1024].bitcast(F32).rearrange("p (g m i u) -> p g m u i", g=2, u=2, i=2),
+                     bank[:].rearrange("p (g u m i) -> p g m u i", g=2, u=2, i=2))
 
         def quantise(key, c0, c1):
             nc.vector.quantize_mx(out=codes[key][:, c0:c1].bitcast(FP8X4), scales=scales[key][:, c0:c1],
@@ -179,8 +179,8 @@ def tile_causalselfattention_pa_t_kernel(tc, x, wk_bytes, wk_scale, pk_w, pk_b, 
             bank = psum.tile([P, 512], F32, name="bank")
             for t in range(4):
                 mx_pass(bank[:, t * P:(t + 1) * P], ("X", unit), t * P, ("W", 0), h * D, D, True, True)
-            copy_out(on_vector, grouped[key][:, h * 512:(h + 1) * 512].rearrange("p (n t) -> p n t", t=4),
-                     bank[:].rearrange("p (t n) -> p n t", t=4))
+            copy_out(on_vector, grouped[key][:, h * 512:(h + 1) * 512].rearrange("p (n i t) -> p n t i", t=4, i=2),
+                     bank[:].rearrange("p (t n i) -> p n t i", t=4, i=2))
 
         def out_tile(pair):
             if pair not in otiles:

@@ -26,7 +26,7 @@ VECTOR_EVERY = 4
 VECTOR_FROM = 11
 TURN_DELAY = 2
 PROJECT_DELAY = 1
-SORT_LEAD = 9
+SORT_LEAD = 10
 UNSORTED = 6
 
 
@@ -61,6 +61,11 @@ def tensor_jobs():
     return jobs
 
 
+MERGED = {}
+SORTED = "X2 X3 X4 X5 X6 X7 P1 P2 P3 P4 P5 P6 P7".split()
+GSORTED = "".split()
+
+
 def tile_causalselfattention_pa_t_kernel(tc, x, wk_bytes, wk_scale, pk_w, pk_b, out):
     nc = tc.nc
     jobs = tensor_jobs()
@@ -79,7 +84,7 @@ def tile_causalselfattention_pa_t_kernel(tc, x, wk_bytes, wk_scale, pk_w, pk_b, 
         ws = keep.tile([P, 4], F32, name="ws", align_bytes=64)
         nc.scalar.dma_start(out=ws[:], in_=wk_scale.rearrange("o (p t) -> p (o t)", t=4))
 
-        raw = {}
+        raw, whole = {}, {}
 
         def load(key, pieces):
             kind, i = key
@@ -94,6 +99,7 @@ def tile_causalselfattention_pa_t_kernel(tc, x, wk_bytes, wk_scale, pk_w, pk_b, 
             for s in range(pieces):
                 t = keep.tile([P, w], BF16, name="raw%s%d_%d" % (kind, i, s), align_bytes=64)
                 nc.sync.dma_start(out=t[:], in_=src[:, s * w:(s + 1) * w])
+                whole[key] = t[:].bitcast(F32)
                 for a in range(2 // pieces):
                     raw[key, s + a] = t[:, a * 1024:(a + 1) * 1024].bitcast(F32)
 
@@ -111,12 +117,18 @@ def tile_causalselfattention_pa_t_kernel(tc, x, wk_bytes, wk_scale, pk_w, pk_b, 
             nc.vector.tensor_copy(out=wv[:, 2 * a:2 * a + 2, :].rearrange("p i k -> p (i k)"),
                                   in_=wb[a][:].rearrange("p i k -> p (i k)").bitcast(FP8))
 
+        big = {}
         grouped, codes, scales, words, otiles = {}, {}, {}, {}, {}
 
         def new_operand(key):
-            grouped[key] = work.tile([P, 2048], BF16, name="grouped", bufs=6, align_bytes=64)
-            codes[key] = keep.tile([P, 512], U32, name="codes%s%d" % key, align_bytes=64)
-            scales[key] = keep.tile([P, 512], U8, name="scales%s%d" % key, align_bytes=64)
+            lead, idx, cnt = MERGED.get(key, (key, 0, 1))
+            if idx == 0:
+                big["g", lead] = work.tile([P, 2048 * cnt], BF16, name="grouped%d" % cnt, bufs=3 if cnt == 2 else 6, align_bytes=64)
+                big["c", lead] = keep.tile([P, 512 * cnt], U32, name="codes%s%d" % key, align_bytes=64)
+                big["s", lead] = keep.tile([P, 512 * cnt], U8, name="scales%s%d" % key, align_bytes=64)
+            grouped[key] = big["g", lead][:, 2048 * idx:2048 * (idx + 1)]
+            codes[key] = big["c", lead][:, 512 * idx:512 * (idx + 1)]
+            scales[key] = big["s", lead][:, 512 * idx:512 * (idx + 1)]
 
         def copy_out(on_vector, dst, src):
             if on_vector:
@@ -124,11 +136,13 @@ def tile_causalselfattention_pa_t_kernel(tc, x, wk_bytes, wk_scale, pk_w, pk_b, 
             else:
                 nc.scalar.copy(out=dst, in_=src)
 
-        def sort(key, a):
-            d = work.tile([P, 4, P], F32, name="sorted", bufs=10, align_bytes=64)
-            nc.vector.tensor_copy(out=d[:].rearrange("p (g u) (m i) -> p g m u i", g=2, i=4),
-                                  in_=raw[key, a].rearrange("p (g m i u) -> p g m u i", g=2, u=2, i=4))
-            words[key, a] = [d[:, n, :] for n in range(4)]
+        def sort(key):
+            d = work.tile([P, 8, P], F32, name="sorted", bufs=5, align_bytes=64)
+            eng = nc.gpsimd if "%s%d" % key in GSORTED else nc.vector
+            eng.tensor_copy(out=d[:].rearrange("p (g u) (m i) -> p g m u i", u=2, i=4),
+                            in_=whole[key].rearrange("p (g m i u) -> p g m u i", g=4, u=2, i=4))
+            for a in range(2):
+                words[key, a] = [d[:, 4 * a + n, :] for n in range(4)]
 
         def turn(key, a, on_vector):
             if a == 0:
@@ -143,8 +157,12 @@ def tile_causalselfattention_pa_t_kernel(tc, x, wk_bytes, wk_scale, pk_w, pk_b, 
                      bank[:].rearrange("p (g u m i) -> p g m u i", g=2, u=2, i=2))
 
         def quantise(key, c0, c1):
-            nc.vector.quantize_mx(out=codes[key][:, c0:c1].bitcast(FP8X4), scales=scales[key][:, c0:c1],
-                                  in_=grouped[key][:, 4 * c0:4 * c1])
+            lead, idx, cnt = MERGED.get(key, (key, 0, 1))
+            if cnt == 1:
+                nc.vector.quantize_mx(out=codes[key][:, c0:c1].bitcast(FP8X4), scales=scales[key][:, c0:c1],
+                                      in_=grouped[key][:, 4 * c0:4 * c1])
+            elif idx == cnt - 1:
+                nc.vector.quantize_mx(out=big["c", lead][:].bitcast(FP8X4), scales=big["s", lead][:], in_=big["g", lead][:])
 
         def turn_w(a):
             key = ("W", 0)
@@ -223,30 +241,60 @@ def tile_causalselfattention_pa_t_kernel(tc, x, wk_bytes, wk_scale, pk_w, pk_b, 
             src = otiles[pair][:].rearrange("p h j d -> p h (j d)")
             nc.sync.dma_start(out=dst[:, h0:h1, j0 * D:j1 * D], in_=src[:, h0:h1, j0 * D:j1 * D])
 
-        to_sort = turn_jobs[UNSORTED:]
-        alternate_from = len(jobs) - 16
-        due = []
+        to_sort = [job for job in turn_jobs[::2] if "%s%d" % job[1] in SORTED]
+        given = {"vector": 6, "scalar": 2}
+        filled = {}
+        waiting = []
+
+        def operands(job):
+            if job[0] == "project":
+                return [("X", job[1]), ("W", 0)]
+            if job[0] == "mix":
+                return [("P", 4 * (job[1] // 2) + job[2] // 2), ("K", 2 * job[1]), ("K", 2 * job[1] + 1)]
+            if job[0] == "mix_half":
+                return [("P", 4 * (job[1] // 2) + job[3] // 2), ("K", 2 * job[1]), ("K", 2 * job[1] + 1)]
+            return []
+
+        def emit_quantise(entry):
+            waiting.remove(entry)
+            quantise(*entry[1:])
+            given["vector"] += (entry[3] - entry[2]) / 512
+
         for n, job in enumerate(jobs):
+            soon = [key for ahead in jobs[n:n + 2] for key in operands(ahead)]
+            for entry in list(waiting):
+                if entry[1] in soon:
+                    emit_quantise(entry)
             if to_sort and to_sort[0] in jobs[n:n + SORT_LEAD + 1]:
-                sort(*to_sort.pop(0)[1:])
-            if n < alternate_from:
-                on_vector = n >= VECTOR_FROM and (n - VECTOR_FROM) % VECTOR_EVERY == 0
-            else:
-                on_vector = (n - alternate_from) % 2 == 0
+                sort(to_sort.pop(0)[1])
+                given["vector"] += 1
+            for entry in list(waiting):
+                if entry[0] <= given["vector"]:
+                    emit_quantise(entry)
             kind = job[0]
+            on_vector = given["vector"] + 0 <= given["scalar"] and n >= 8
+            if n >= len(jobs) - 6:
+                on_vector = (len(jobs) - n) % 2 == 1
+            engine = "vector" if on_vector else "scalar"
+            if kind != "turn_w":
+                given[engine] = max(given[engine], min(given.values())) + 1
+            ready = given[engine] + 0.5
             if kind == "turn_w":
                 turn_w(job[1])
-                due.append((n + TURN_DELAY, ("W", 0), 256 * job[1], 256 * (job[1] + 1)))
+                if job[1] == 1:
+                    waiting.extend([(0, ("W", 0), 0, 256), (0, ("W", 0), 256, 512)])
             elif kind == "turn":
                 turn(job[1], job[2], on_vector)
+                filled[job[1]] = max(filled.get(job[1], 0), ready)
                 if job[2] == 1:
-                    due.append((n + TURN_DELAY, job[1], 0, 512))
+                    waiting.append((filled[job[1]], job[1], 0, 512))
             elif kind == "project":
                 unit, h = job[1:]
                 project(unit, h, on_vector)
+                filled["K", unit] = max(filled.get(("K", unit), 0), ready)
                 heads = 2 if unit // 2 == PAIRS - 1 else NH
                 if (h + 1) % heads == 0:
-                    due.append((n + PROJECT_DELAY, ("K", unit), (h + 1 - heads) * D, (h + 1) * D))
+                    waiting.append((filled["K", unit], ("K", unit), (h + 1 - heads) * D, (h + 1) * D))
             elif kind == "mix":
                 pair, j = job[1:]
                 mix(pair, j, on_vector)
@@ -259,6 +307,3 @@ def tile_causalselfattention_pa_t_kernel(tc, x, wk_bytes, wk_scale, pk_w, pk_b, 
                 rows = 2 if n >= len(jobs) - 2 else 4
                 if (j0 + 2) % rows == 0:
                     store(pair, h0, h0 + 2, j0 + 2 - rows, j0 + 2)
-            for entry in [entry for entry in due if entry[0] <= n]:
-                due.remove(entry)
-                quantise(*entry[1:])

@@ -26,7 +26,7 @@ VECTOR_EVERY = 4
 VECTOR_FROM = 11
 TURN_DELAY = 2
 PROJECT_DELAY = 1
-SORT_LEAD = 10
+SORT_LEAD = 7
 UNSORTED = 6
 
 
@@ -34,30 +34,26 @@ def tensor_jobs():
     def turn(*keys):
         return [("turn", key, a) for key in keys for a in range(2)]
 
-    def project(unit, heads):
+    def project(unit, *heads):
         return [("project", unit, h) for h in heads]
 
+    def mix(pair, *rows):
+        return [("mix", pair, j) for j in rows]
+
     jobs = [("turn_w", a) for a in range(2)] + turn(("X", 0), ("X", 1), ("P", 0))
-    jobs += project(0, range(NH)) + project(1, range(NH))
-    turns = [[("P", 1), ("X", 2), ("X", 3), ("P", 2), ("P", 3)],
-             [("X", 4), ("X", 5), ("P", 4), ("P", 5)],
-             [("X", 6), ("X", 7), ("P", 6), ("P", 7)]]
-    for pair in range(PAIRS - 2):
-        jobs += turn(*turns[pair])
-        mixes = [("mix", pair, j) for j in range(ROWS)]
-        projections = project(2 * pair + 2, range(NH)) + project(2 * pair + 3, range(NH))
-        jobs += mixes[:2]
-        for n in range(4):
-            jobs += projections[2 * n:2 * n + 2] + [mixes[2 + n]]
-        jobs += mixes[6:]
-    jobs += turn(*turns[2])
-    mixes = [("mix", 2, j) for j in range(ROWS)]
-    mixes += [("mix_half", 3, h0, j0) for h0 in (0, 2) for j0 in range(0, ROWS, 2)]
-    projections = [job for h0 in (0, 2) for unit in (6, 7) for job in project(unit, (h0, h0 + 1))]
-    jobs += mixes[:2]
-    for n, job in enumerate(projections):
-        jobs += [job, mixes[2 + n]]
-    jobs += mixes[2 + len(projections):]
+    jobs += project(0, 0, 1, 2, 3) + project(1, 0, 1, 2, 3)
+    jobs += turn(("X", 2), ("P", 1), ("P", 2))
+    jobs += mix(0, 0, 1) + project(2, 0, 1) + mix(0, 2) + project(2, 2, 3) + mix(0, 3)
+    jobs += turn(("X", 3), ("P", 3), ("X", 4))
+    jobs += mix(0, 4, 5) + project(3, 0, 1, 2, 3) + mix(0, 6, 7)
+    jobs += turn(("X", 5), ("P", 4), ("P", 5))
+    jobs += project(4, 0, 1) + mix(1, 0) + project(4, 2, 3) + mix(1, 1, 2)
+    jobs += project(5, 0, 1) + mix(1, 3) + project(5, 2, 3) + mix(1, 4, 5, 6, 7)
+    jobs += turn(("X", 6), ("X", 7), ("P", 6), ("P", 7))
+    jobs += mix(2, 0, 1) + project(6, 0) + mix(2, 2) + project(6, 1) + mix(2, 3) + project(7, 0) + mix(2, 4)
+    jobs += project(7, 1) + mix(2, 5) + project(6, 2) + mix(2, 6) + project(6, 3) + mix(2, 7) + project(7, 2)
+    halves = [("mix_half", 3, h0, j0) for h0 in (0, 2) for j0 in range(0, ROWS, 2)]
+    jobs += halves[:1] + project(7, 3) + halves[1:-1] + [("mix_row", 3, 2, j) for j in (ROWS - 2, ROWS - 1)]
     return jobs
 
 
@@ -79,10 +75,10 @@ def tile_causalselfattention_pa_t_kernel(tc, x, wk_bytes, wk_scale, pk_w, pk_b, 
         wb = []
         for a in range(2):
             t = keep.tile([P, 2, C], U8, name="wb%d" % a, align_bytes=64)
-            nc.sync.dma_start(out=t[:], in_=wk_bytes.rearrange("(i r) k -> r i k", r=P)[:, 2 * a:2 * a + 2, :])
+            nc.sync.dma_start(out=t[:], in_=wk_bytes.rearrange("(r i) k -> r i k", i=4)[:, 2 * a:2 * a + 2, :])
             wb.append(t)
-        ws = keep.tile([P, 4], F32, name="ws", align_bytes=64)
-        nc.scalar.dma_start(out=ws[:], in_=wk_scale.rearrange("o (p t) -> p (o t)", t=4))
+        ws = keep.tile([P, 2, 4], F32, name="ws", align_bytes=64)
+        nc.scalar.dma_start(out=ws[:], in_=wk_scale.rearrange("o (p t) -> p o t", t=4).to_broadcast([P, 2, 4]))
 
         raw, whole = {}, {}
 
@@ -106,7 +102,7 @@ def tile_causalselfattention_pa_t_kernel(tc, x, wk_bytes, wk_scale, pk_w, pk_b, 
         bias = keep.tile([P, NC, ROWS], BF16, name="bias", align_bytes=64)
         for n, job in enumerate(turn_jobs[::2]):
             load(job[1], 2 if n == 0 else 1)
-            if n == 3:
+            if n == 7:
                 nc.sync.dma_start(out=bias[:], in_=pk_b.rearrange("c (p j) -> p c j", j=ROWS))
 
         ident = keep.tile([P, P], F32, name="ident", align_bytes=64)
@@ -174,14 +170,11 @@ def tile_causalselfattention_pa_t_kernel(tc, x, wk_bytes, wk_scale, pk_w, pk_b, 
                 for u in range(2):
                     n = 2 * i + u
                     nc.tensor.transpose(bank[:, n * P:(n + 1) * P], ww[:, u:256:2], ident[:])
-            vals = bank[:].bitcast(BF16)
-            for i in range(2):
-                base = (2 * a + i) * 512
-                nc.vector.tensor_tensor(
-                    out=grouped[key][:, base:base + 512].rearrange("p (r u e) -> p r u e", u=2, e=2),
-                    in0=vals[:, i * 512:(i + 1) * 512].rearrange("p (u r e) -> p r u e", u=2, e=2),
-                    in1=ws[:].rearrange("p (u e) -> p u e", u=2).unsqueeze(1).to_broadcast([P, P, 2, 2]),
-                    op=MULT)
+            nc.vector.tensor_tensor(
+                out=grouped[key].rearrange("p (r a n e) -> p r a n e", a=2, n=4, e=2)[:, :, a],
+                in0=bank[:].bitcast(BF16).rearrange("p (n r e) -> p r n e", n=4, e=2),
+                in1=ws[:].rearrange("p i (u e) -> p (i u) e", e=2).unsqueeze(1).to_broadcast([P, P, 4, 2]),
+                op=MULT)
 
         def mx_pass(dst, stationary, s0, moving, m0, width, start, stop):
             nc.tensor.matmul_mx(
@@ -235,6 +228,17 @@ def tile_causalselfattention_pa_t_kernel(tc, x, wk_bytes, wk_scale, pk_w, pk_b, 
                 for jj in range(2):
                     nc.scalar.activation(out=dst[:, jj], in_=src[:, jj], func=IDENT, bias=columns[:, jj:jj + 1])
 
+        def mix_row(pair, h0, j, on_vector):
+            bank = psum.tile([P, 512], F32, name="bank")
+            mix_passes(bank[:, 0:256], pair, j, h0, 2)
+            src = bank[:, 0:256].rearrange("p (h d) -> p h d", d=D)
+            dst = out_tile(pair)[:, h0:h0 + 2, j, :]
+            column = bias[:, pair // 2, j:j + 1]
+            if on_vector:
+                nc.vector.tensor_scalar(out=dst, in0=src, scalar1=column, scalar2=None, op0=ADD)
+            else:
+                nc.scalar.activation(out=dst, in_=src, func=IDENT, bias=column)
+
         def store(pair, h0, h1, j0, j1):
             c, b = divmod(pair, 2)
             dst = out[b, :, c * N:(c + 1) * N, :].rearrange("h (p j) d -> p h (j d)", j=ROWS)
@@ -251,7 +255,7 @@ def tile_causalselfattention_pa_t_kernel(tc, x, wk_bytes, wk_scale, pk_w, pk_b, 
                 return [("X", job[1]), ("W", 0)]
             if job[0] == "mix":
                 return [("P", 4 * (job[1] // 2) + job[2] // 2), ("K", 2 * job[1]), ("K", 2 * job[1] + 1)]
-            if job[0] == "mix_half":
+            if job[0] in ("mix_half", "mix_row"):
                 return [("P", 4 * (job[1] // 2) + job[3] // 2), ("K", 2 * job[1]), ("K", 2 * job[1] + 1)]
             return []
 
@@ -272,9 +276,9 @@ def tile_causalselfattention_pa_t_kernel(tc, x, wk_bytes, wk_scale, pk_w, pk_b, 
                 if entry[0] <= given["vector"]:
                     emit_quantise(entry)
             kind = job[0]
-            on_vector = given["vector"] + 0 <= given["scalar"] and n >= 8
-            if n >= len(jobs) - 6:
-                on_vector = (len(jobs) - n) % 2 == 1
+            on_vector = given["vector"] + (0 if kind.startswith("mix") else 0) <= given["scalar"] and n >= 8
+            if n >= len(jobs) - 7:
+                on_vector = (len(jobs) - n) % 2 == 0
             engine = "vector" if on_vector else "scalar"
             if kind != "turn_w":
                 given[engine] = max(given[engine], min(given.values())) + 1
@@ -282,7 +286,7 @@ def tile_causalselfattention_pa_t_kernel(tc, x, wk_bytes, wk_scale, pk_w, pk_b, 
             if kind == "turn_w":
                 turn_w(job[1])
                 if job[1] == 1:
-                    waiting.extend([(0, ("W", 0), 0, 256), (0, ("W", 0), 256, 512)])
+                    waiting.append((0, ("W", 0), 0, 512))
             elif kind == "turn":
                 turn(job[1], job[2], on_vector)
                 filled[job[1]] = max(filled.get(job[1], 0), ready)
@@ -301,9 +305,14 @@ def tile_causalselfattention_pa_t_kernel(tc, x, wk_bytes, wk_scale, pk_w, pk_b, 
                 rows = 2 if pair == PAIRS - 2 else 4
                 if (j + 1) % rows == 0:
                     store(pair, 0, NH, j + 1 - rows, j + 1)
+            elif kind == "mix_row":
+                pair, h0, j = job[1:]
+                mix_row(pair, h0, j, on_vector)
+                if j % 2 == 1:
+                    store(pair, h0, h0 + 2, j + 1 - 2, j + 1)
             else:
                 pair, h0, j0 = job[1:]
                 mix_half(pair, h0, j0, on_vector)
-                rows = 2 if n >= len(jobs) - 2 else 4
+                rows = 2 if n >= len(jobs) - 3 or (h0 == 0 and j0 < 4) else 4
                 if (j0 + 2) % rows == 0:
                     store(pair, h0, h0 + 2, j0 + 2 - rows, j0 + 2)

@@ -120,8 +120,10 @@ def tile_causalselfattention_pa_t_kernel(tc, x, wk_bytes, wk_scale, pk_w, pk_b, 
             lead, idx, cnt = MERGED.get(key, (key, 0, 1))
             if idx == 0:
                 big["g", lead] = work.tile([P, 2048 * cnt], BF16, name="grouped%d" % cnt, bufs=3 if cnt == 2 else 6, align_bytes=64)
-                big["c", lead] = keep.tile([P, 512 * cnt], U32, name="codes%s%d" % key, align_bytes=64)
-                big["s", lead] = keep.tile([P, 512 * cnt], U8, name="scales%s%d" % key, align_bytes=64)
+                moving = key[0] in "WK"
+                c0, s0 = (0, 64) if moving else (128, 192)
+                big["c", lead] = keep.tile([P, 512 * cnt + 64], U32, name="codes%s%d" % key, align_bytes=256)[:, c0 // 4:c0 // 4 + 512 * cnt]
+                big["s", lead] = keep.tile([P, 512 * cnt + 256], U8, name="scales%s%d" % key, align_bytes=256)[:, s0:s0 + 512 * cnt]
             grouped[key] = big["g", lead][:, 2048 * idx:2048 * (idx + 1)]
             codes[key] = big["c", lead][:, 512 * idx:512 * (idx + 1)]
             scales[key] = big["s", lead][:, 512 * idx:512 * (idx + 1)]

@@ -22,68 +22,85 @@ P = 128
 BANKS = 8
 ROWS = N // P
 PAIRS = B * NC
-VECTOR_EVERY = 4
-VECTOR_FROM = 11
-TURN_DELAY = 2
-PROJECT_DELAY = 1
-SORT_LEAD = 7
-UNSORTED = 6
+LAST = PAIRS - 1
+SPLIT = ["X0"]
+BIAS_AFTER = 9
+SLOTS = 11
+DEPTH = {"W": 1, "X": 4, "P": 6, "K": 5}
+STORE_ROWS = [(4, 4), (4, 4), (2, 2)]
+OBUFS = 7
+QUARTERED = [1]
 
 
-def tensor_jobs():
-    def turn(*keys):
-        return [("turn", key, a) for key in keys for a in range(2)]
+def program():
+    def banks(jobs, engines):
+        assert len(jobs) == len(engines)
+        return [job + (e == "V",) for job, e in zip(jobs, engines)]
 
-    def project(unit, *heads):
-        return [("project", unit, h) for h in heads]
+    def turn(keys, engines):
+        return banks([("turn", key, a) for key in keys.split() for a in range(2)], engines)
 
-    def mix(pair, *rows):
-        return [("mix", pair, j) for j in rows]
+    def project(unit, heads, engines):
+        return banks([("project", unit, h) for h in heads], engines)
 
-    jobs = [("turn_w", a) for a in range(2)] + turn(("X", 0), ("X", 1), ("P", 0))
-    jobs += project(0, 0, 1, 2, 3) + project(1, 0, 1, 2, 3)
-    jobs += turn(("X", 2), ("P", 1), ("P", 2))
-    jobs += mix(0, 0, 1) + project(2, 0, 1) + mix(0, 2) + project(2, 2, 3) + mix(0, 3)
-    jobs += turn(("X", 3), ("P", 3), ("X", 4))
-    jobs += mix(0, 4, 5) + project(3, 0, 1, 2, 3) + mix(0, 6, 7)
-    jobs += turn(("X", 5), ("P", 4), ("P", 5))
-    jobs += project(4, 0, 1) + mix(1, 0) + project(4, 2, 3) + mix(1, 1, 2)
-    jobs += project(5, 0, 1) + mix(1, 3) + project(5, 2, 3) + mix(1, 4, 5, 6, 7)
-    jobs += turn(("X", 6), ("X", 7), ("P", 6), ("P", 7))
-    jobs += mix(2, 0, 1) + project(6, 0) + mix(2, 2) + project(6, 1) + mix(2, 3) + project(7, 0) + mix(2, 4)
-    jobs += project(7, 1) + mix(2, 5) + project(6, 2) + mix(2, 6) + project(6, 3) + mix(2, 7) + project(7, 2)
-    halves = [("mix_half", 3, h0, j0) for h0 in (0, 2) for j0 in range(0, ROWS, 2)]
-    jobs += halves[:1] + project(7, 3) + halves[1:-1] + [("mix_row", 3, 2, j) for j in (ROWS - 2, ROWS - 1)]
+    def both(h, engines):
+        return banks([("project", 2 * LAST + u, h) for u in range(2)], engines)
+
+    def mix(pair, rows, engines):
+        return banks([("mix", pair, j) for j in rows], engines)
+
+    def mix_head(h, spans, engines):
+        return banks([("mix_head", h, j0, j1) for j0, j1 in spans], engines)
+
+    def quantise(keys):
+        return [("quantise", key, 0, 512) for key in keys.split()]
+
+    def quantise_half(key, a):
+        return [("quantise", key, 256 * a, 256 * (a + 1))]
+
+    def sort(keys):
+        return [("sort", key, n == 0) for n, key in enumerate(keys.split())]
+
+    def vsort(keys):
+        return [("vsort", key) for key in keys.split()]
+
+    jobs = [("turn_w", 0), ("turn_w", 1)] + turn("X0 X1 P0", "SSSSSS")
+    jobs += quantise_half("W0", 0) + quantise("X0") + quantise_half("W0", 1) + quantise("X1") + sort("X2 P1")
+    jobs += project(0, range(4), "VSVS") + project(1, range(4), "VSVS")
+    jobs += quantise("P0 K0 K1") + turn("X2 P1", "SSSS") + quantise("X2") + vsort("X3") + quantise("P1") + sort("P3 X4") + turn("P2", "SV")
+    jobs += mix(0, (0, 1), "SV") + project(2, (0, 1), "SV") + mix(0, (2,), "S") + project(2, (2, 3), "VS") + quantise("P2") + mix(0, (3,), "S")
+    jobs += vsort("P5") + turn("X3 P3", "SVSS") + quantise("X3 P3") + sort("X5 P4") + turn("X4", "SV")
+    jobs += mix(0, (4, 5), "SV") + project(3, range(4), "SVSV") + quantise("X4 K2") + mix(0, (6, 7), "SS")
+    jobs += quantise("K3") + turn("X5 P5 P4", "SVSVSS") + quantise("X5 P5") + sort("X6 X7 P6")
+    jobs += project(4, (0, 1), "SV") + mix(1, (0,), "S") + project(4, (2, 3), "VS") + mix(1, (1, 2), "VS")
+    jobs += project(5, (0, 1), "SV") + mix(1, (3,), "S") + project(5, (2, 3), "VS") + mix(1, (4,), "V") + vsort("P7") + quantise("P4 K4 K5") + mix(1, (5, 6, 7), "SSS")
+    jobs += turn("X6 X7", "SVSS") + quantise("X6") + turn("P6", "VS") + quantise("X7") + turn("P7", "SS") + quantise("P6")
+    jobs += mix(2, (0, 1), "SV") + quantise("P7") + mix(2, (2,), "S") + both(0, "SV") + mix(2, (3,), "S") + both(1, "VS") + mix(2, (4, 5), "VS") + quantise("H0") + mix(2, (6, 7), "SV")
+    jobs += both(2, "SV") + mix_head(0, [(0, 2)], "S") + both(3, "VS") + quantise_half("H1", 0) + mix_head(0, [(2, 4), (4, 6)], "SV") + quantise_half("H1", 1) + mix_head(0, [(6, 8)], "S")
+    jobs += mix_head(2, [(0, 4), (4, 8)], "VV") + mix_head(3, [(0, 4), (4, 6), (6, 8)], "VSV")
     return jobs
-
-
-MERGED = {}
-SORTED = "X2 X3 X4 X5 X6 X7 P1 P2 P3 P4 P5 P6 P7".split()
-GSORTED = "".split()
 
 
 def tile_causalselfattention_pa_t_kernel(tc, x, wk_bytes, wk_scale, pk_w, pk_b, out):
     nc = tc.nc
-    jobs = tensor_jobs()
-    turn_jobs = [job for job in jobs if job[0] == "turn"]
+    jobs = program()
     with ExitStack() as ctx:
         keep = ctx.enter_context(tc.tile_pool(name="keep", bufs=1))
         work = ctx.enter_context(tc.tile_pool(name="work", bufs=1))
         psum = ctx.enter_context(tc.psum_pool(name="psum", bufs=BANKS))
         ctx.enter_context(tc.manual_schedule())
 
-        wb = []
-        for a in range(2):
-            t = keep.tile([P, 2, C], U8, name="wb%d" % a, align_bytes=64)
-            nc.sync.dma_start(out=t[:], in_=wk_bytes.rearrange("(r i) k -> r i k", i=4)[:, 2 * a:2 * a + 2, :])
-            wb.append(t)
-        ws = keep.tile([P, 2, 4], F32, name="ws", align_bytes=64)
-        nc.scalar.dma_start(out=ws[:], in_=wk_scale.rearrange("o (p t) -> p o t", t=4).to_broadcast([P, 2, 4]))
+        ws = keep.tile([P, 4], F32, name="ws", align_bytes=64)
+        nc.scalar.dma_start(out=ws[:], in_=wk_scale.rearrange("o (p t) -> p (o t)", t=4))
 
-        raw, whole = {}, {}
+        wb, raw, whole = {}, {}, {}
+
+        def load_w(a):
+            wb[a] = keep.tile([P, 2, C], U8, name="wb%d" % a, align_bytes=64)
+            nc.sync.dma_start(out=wb[a][:], in_=wk_bytes.rearrange("(h r) k -> r h k", h=NH)[:, 2 * a:2 * a + 2, :])
 
         def load(key, pieces):
-            kind, i = key
+            kind, i = key[0], int(key[1])
             if kind == "X":
                 c, b, u = i // 4, i // 2 % 2, i % 2
                 r0 = c * N + u * 512
@@ -100,33 +117,33 @@ def tile_causalselfattention_pa_t_kernel(tc, x, wk_bytes, wk_scale, pk_w, pk_b, 
                     raw[key, s + a] = t[:, a * 1024:(a + 1) * 1024].bitcast(F32)
 
         bias = keep.tile([P, NC, ROWS], BF16, name="bias", align_bytes=64)
-        for n, job in enumerate(turn_jobs[::2]):
-            load(job[1], 2 if n == 0 else 1)
-            if n == 7:
+        loads = [job for job in jobs if job[0] == "turn_w" or job[0] == "turn" and job[2] == 0]
+        load_w(0)
+        load_w(1)
+        for n, job in enumerate(loads):
+            if job[0] != "turn_w":
+                load(job[1], 2 if job[1] in SPLIT else 1)
+            if n == BIAS_AFTER:
                 nc.sync.dma_start(out=bias[:], in_=pk_b.rearrange("c (p j) -> p c j", j=ROWS))
 
         ident = keep.tile([P, P], F32, name="ident", align_bytes=64)
         make_identity(nc, ident[:])
 
-        wv = keep.tile([P, 4, C], BF16, name="wv", align_bytes=64)
-        for a in range(2):
-            nc.vector.tensor_copy(out=wv[:, 2 * a:2 * a + 2, :].rearrange("p i k -> p (i k)"),
-                                  in_=wb[a][:].rearrange("p i k -> p (i k)").bitcast(FP8))
+        grouped, codes, scales, words, otiles, wv = {}, {}, {}, {}, {}, {}
+        free_slots = list(range(SLOTS))
+        slot_of = {}
 
-        big = {}
-        grouped, codes, scales, words, otiles = {}, {}, {}, {}, {}
+        def take_slot(owner, shape, dtype, newest):
+            slot_of[owner] = free_slots.pop(-1 if newest else 0)
+            return work.tile(shape, dtype, name="slot%d" % slot_of[owner], align_bytes=64)
 
         def new_operand(key):
-            lead, idx, cnt = MERGED.get(key, (key, 0, 1))
-            if idx == 0:
-                big["g", lead] = work.tile([P, 2048 * cnt], BF16, name="grouped%d" % cnt, bufs=3 if cnt == 2 else 6, align_bytes=64)
-                moving = key[0] in "WK"
-                c0, s0 = (0, 64) if moving else (128, 192)
-                big["c", lead] = keep.tile([P, 512 * cnt + 64], U32, name="codes%s%d" % key, align_bytes=256)[:, c0 // 4:c0 // 4 + 512 * cnt]
-                big["s", lead] = keep.tile([P, 512 * cnt + 256], U8, name="scales%s%d" % key, align_bytes=256)[:, s0:s0 + 512 * cnt]
-            grouped[key] = big["g", lead][:, 2048 * idx:2048 * (idx + 1)]
-            codes[key] = big["c", lead][:, 512 * idx:512 * (idx + 1)]
-            scales[key] = big["s", lead][:, 512 * idx:512 * (idx + 1)]
+            grouped[key] = take_slot(key, [P, 2048], BF16, False)[:]
+            moving = key[0] in "WKH"
+            c0, s0 = (0, 64) if moving else (128, 192)
+            kind = "K" if key[0] == "H" else key[0]
+            codes[key] = work.tile([P, 512 + 64], U32, name="codes" + kind, bufs=DEPTH[kind], align_bytes=256)[:, c0 // 4:c0 // 4 + 512]
+            scales[key] = work.tile([P, 512 + 256], U8, name="scales" + kind, bufs=DEPTH[kind], align_bytes=256)[:, s0:s0 + 512]
 
         def copy_out(on_vector, dst, src):
             if on_vector:
@@ -134,13 +151,25 @@ def tile_causalselfattention_pa_t_kernel(tc, x, wk_bytes, wk_scale, pk_w, pk_b, 
             else:
                 nc.scalar.copy(out=dst, in_=src)
 
-        def sort(key):
-            d = work.tile([P, 8, P], F32, name="sorted", bufs=5, align_bytes=64)
-            eng = nc.gpsimd if "%s%d" % key in GSORTED else nc.vector
-            eng.tensor_copy(out=d[:].rearrange("p (g u) (m i) -> p g m u i", u=2, i=4),
-                            in_=whole[key].rearrange("p (g m i u) -> p g m u i", g=4, u=2, i=4))
+        def widen(a):
+            wv[a] = keep.tile([P, 2 * C], BF16, name="wv%d" % a, align_bytes=64)
+            nc.vector.tensor_copy(out=wv[a][:], in_=wb[a][:].rearrange("p i k -> p (i k)").bitcast(FP8))
+
+        def sorted_tile(key, newest):
+            d = take_slot(("sorted", key), [P, 8, P], F32, newest)
             for a in range(2):
                 words[key, a] = [d[:, 4 * a + n, :] for n in range(4)]
+            return d
+
+        def sort(key, first):
+            d = sorted_tile(key, first)
+            nc.gpsimd.tensor_copy(out=d[:].rearrange("p (g u) m -> p g u m", u=2),
+                                  in_=whole[key].rearrange("p (g m u) -> p g u m", g=4, u=2))
+
+        def vsort(key):
+            d = sorted_tile(key, False)
+            nc.vector.tensor_copy(out=d[:].rearrange("p (g u) (m i) -> p g m u i", u=2, i=4),
+                                  in_=whole[key].rearrange("p (g m i u) -> p g m u i", g=4, u=2, i=4))
 
         def turn(key, a, on_vector):
             if a == 0:
@@ -150,32 +179,32 @@ def tile_causalselfattention_pa_t_kernel(tc, x, wk_bytes, wk_scale, pk_w, pk_b, 
             bank = psum.tile([P, 512], F32, name="bank")
             for n in range(4):
                 nc.tensor.transpose(bank[:, n * P:(n + 1) * P], src[n], ident[:])
+            if a == 1 and ("sorted", key) in slot_of:
+                free_slots.append(slot_of["sorted", key])
             copy_out(on_vector,
                      grouped[key][:, a * 1024:(a + 1) * 1024].bitcast(F32).rearrange("p (g m i u) -> p g m u i", g=2, u=2, i=2),
                      bank[:].rearrange("p (g u m i) -> p g m u i", g=2, u=2, i=2))
 
         def quantise(key, c0, c1):
-            lead, idx, cnt = MERGED.get(key, (key, 0, 1))
-            if cnt == 1:
-                nc.vector.quantize_mx(out=codes[key][:, c0:c1].bitcast(FP8X4), scales=scales[key][:, c0:c1],
-                                      in_=grouped[key][:, 4 * c0:4 * c1])
-            elif idx == cnt - 1:
-                nc.vector.quantize_mx(out=big["c", lead][:].bitcast(FP8X4), scales=big["s", lead][:], in_=big["g", lead][:])
+            nc.vector.quantize_mx(out=codes[key][:, c0:c1].bitcast(FP8X4), scales=scales[key][:, c0:c1],
+                                  in_=grouped[key][:, 4 * c0:4 * c1])
+            if c1 == 512:
+                free_slots.append(slot_of[key])
 
         def turn_w(a):
-            key = ("W", 0)
+            key = "W0"
             if a == 0:
                 new_operand(key)
             bank = psum.tile([P, 512], F32, name="bank")
-            for i in range(2):
-                ww = wv[:, 2 * a + i, :].bitcast(F32)
-                for u in range(2):
-                    n = 2 * i + u
-                    nc.tensor.transpose(bank[:, n * P:(n + 1) * P], ww[:, u:256:2], ident[:])
+            ww = wv[a][:].bitcast(F32)
+            for u in range(2):
+                for i in range(2):
+                    n = 2 * u + i
+                    nc.tensor.transpose(bank[:, n * P:(n + 1) * P], ww[:, 256 * i + u:256 * (i + 1):2], ident[:])
             nc.vector.tensor_tensor(
-                out=grouped[key].rearrange("p (r a n e) -> p r a n e", a=2, n=4, e=2)[:, :, a],
-                in0=bank[:].bitcast(BF16).rearrange("p (n r e) -> p r n e", n=4, e=2),
-                in1=ws[:].rearrange("p i (u e) -> p (i u) e", e=2).unsqueeze(1).to_broadcast([P, P, 4, 2]),
+                out=grouped[key][:, a * 1024:(a + 1) * 1024].rearrange("p (c u e) -> p c u e", u=2, e=2),
+                in0=bank[:].bitcast(BF16).rearrange("p (u c e) -> p c u e", u=2, e=2),
+                in1=ws[:].rearrange("p (u e) -> p u e", e=2).unsqueeze(1).to_broadcast([P, 2 * P, 2, 2]),
                 op=MULT)
 
         def mx_pass(dst, stationary, s0, moving, m0, width, start, stop):
@@ -185,136 +214,69 @@ def tile_causalselfattention_pa_t_kernel(tc, x, wk_bytes, wk_scale, pk_w, pk_b, 
                 rhs=codes[moving][:, m0:m0 + width].bitcast(FP8X4), rhs_scale=scales[moving][:, m0:m0 + width],
                 start=start, stop=stop)
 
+        def keys_place(unit, h):
+            if unit // 2 == LAST:
+                return "H%d" % (h // 2), ((h % 2 * 2 + unit % 2) if h // 2 in QUARTERED else (unit % 2 * 2 + h % 2)) * D
+            return "K%d" % unit, h * D
+
         def project(unit, h, on_vector):
-            key = ("K", unit)
-            if h == 0:
+            key, c0 = keys_place(unit, h)
+            if key not in grouped:
                 new_operand(key)
             bank = psum.tile([P, 512], F32, name="bank")
             for t in range(4):
-                mx_pass(bank[:, t * P:(t + 1) * P], ("X", unit), t * P, ("W", 0), h * D, D, True, True)
-            copy_out(on_vector, grouped[key][:, h * 512:(h + 1) * 512].rearrange("p (n i t) -> p n t i", t=4, i=2),
+                mx_pass(bank[:, t * P:(t + 1) * P], "X%d" % unit, t * P, "W0", h * D, D, True, True)
+            copy_out(on_vector, grouped[key][:, 4 * c0:4 * (c0 + D)].rearrange("p (n i t) -> p n t i", t=4, i=2),
                      bank[:].rearrange("p (t n i) -> p n t i", t=4, i=2))
 
-        def out_tile(pair):
-            if pair not in otiles:
-                otiles[pair] = work.tile([P, NH, ROWS, D], F32, name="o", bufs=2, align_bytes=64)
-            return otiles[pair]
-
-        def mix_passes(dst, pair, j, h0, heads):
+        def mix_passes(dst, pair, j, h, heads):
             for u in range(2):
-                mx_pass(dst, ("P", 4 * (pair // 2) + j // 2), (j % 2) * 256 + u * P,
-                        ("K", 2 * pair + u), h0 * D, heads * D, u == 0, u == 1)
+                key, c0 = keys_place(2 * pair + u, h)
+                mx_pass(dst, "P%d" % (4 * (pair // 2) + j // 2), (j % 2) * 256 + u * P, key, c0, heads * D, u == 0, u == 1)
+
+        def hbm_rows(pair):
+            c, b = divmod(pair, 2)
+            return out[b, :, c * N:(c + 1) * N, :].rearrange("h (p j) d -> p h j d", j=ROWS)
 
         def mix(pair, j, on_vector):
+            rows = STORE_ROWS[pair][j // 4]
+            if j % rows == 0:
+                otiles[pair] = work.tile([P, NH, rows, D], F32, name="o", bufs=OBUFS, align_bytes=64)
             bank = psum.tile([P, 512], F32, name="bank")
             mix_passes(bank[:], pair, j, 0, NH)
             src = bank[:].rearrange("p (h d) -> p h d", h=NH)
-            dst = out_tile(pair)[:, :, j, :]
+            dst = otiles[pair][:, :, j % rows, :]
             column = bias[:, pair // 2, j:j + 1]
             if on_vector:
                 nc.vector.tensor_scalar(out=dst, in0=src, scalar1=column, scalar2=None, op0=ADD)
             else:
                 nc.scalar.activation(out=dst, in_=src, func=IDENT, bias=column)
+            if (j + 1) % rows == 0:
+                nc.sync.dma_start(out=hbm_rows(pair)[:, :, j + 1 - rows:j + 1, :].rearrange("p h j d -> p h (j d)"),
+                                  in_=otiles[pair][:].rearrange("p h j d -> p h (j d)"))
 
-        def mix_half(pair, h0, j0, on_vector):
+        def mix_head(h, j0, j1, on_vector):
+            rows = j1 - j0
+            heads = 1 if h // 2 in QUARTERED else 2
+            o = work.tile([P, heads, rows, D], F32, name="o", bufs=OBUFS, align_bytes=64)
             bank = psum.tile([P, 512], F32, name="bank")
-            for jj in range(2):
-                mix_passes(bank[:, jj * 256:(jj + 1) * 256], pair, j0 + jj, h0, 2)
-            src = bank[:].rearrange("p (j h d) -> p j h d", j=2, d=D)
-            dst = out_tile(pair)[:, h0:h0 + 2, j0:j0 + 2, :].rearrange("p h j d -> p j h d")
-            columns = bias[:, pair // 2, j0:j0 + 2]
+            w = heads * D
+            for jj in range(rows):
+                mix_passes(bank[:, jj * w:(jj + 1) * w], LAST, j0 + jj, h, heads)
+            src = bank[:, 0:rows * w].rearrange("p (j h d) -> p j h d", h=heads, d=D)
+            dst = o[:].rearrange("p h j d -> p j h d")
+            columns = bias[:, LAST // 2, j0:j1]
             if on_vector:
-                nc.vector.tensor_tensor(out=dst, in0=src, op=ADD,
-                                        in1=columns.unsqueeze(2).unsqueeze(3).to_broadcast([P, 2, 2, D]))
+                nc.vector.tensor_tensor(out=dst, in0=src, op=ADD, in1=columns.unsqueeze(2).unsqueeze(3).to_broadcast([P, rows, heads, D]))
             else:
-                for jj in range(2):
+                for jj in range(rows):
                     nc.scalar.activation(out=dst[:, jj], in_=src[:, jj], func=IDENT, bias=columns[:, jj:jj + 1])
+            nc.sync.dma_start(out=hbm_rows(LAST)[:, h:h + heads, j0:j1, :].rearrange("p h j d -> p h (j d)"),
+                              in_=o[:].rearrange("p h j d -> p h (j d)"))
 
-        def mix_row(pair, h0, j, on_vector):
-            bank = psum.tile([P, 512], F32, name="bank")
-            mix_passes(bank[:, 0:256], pair, j, h0, 2)
-            src = bank[:, 0:256].rearrange("p (h d) -> p h d", d=D)
-            dst = out_tile(pair)[:, h0:h0 + 2, j, :]
-            column = bias[:, pair // 2, j:j + 1]
-            if on_vector:
-                nc.vector.tensor_scalar(out=dst, in0=src, scalar1=column, scalar2=None, op0=ADD)
-            else:
-                nc.scalar.activation(out=dst, in_=src, func=IDENT, bias=column)
-
-        def store(pair, h0, h1, j0, j1):
-            c, b = divmod(pair, 2)
-            dst = out[b, :, c * N:(c + 1) * N, :].rearrange("h (p j) d -> p h (j d)", j=ROWS)
-            src = otiles[pair][:].rearrange("p h j d -> p h (j d)")
-            nc.sync.dma_start(out=dst[:, h0:h1, j0 * D:j1 * D], in_=src[:, h0:h1, j0 * D:j1 * D])
-
-        to_sort = [job for job in turn_jobs[::2] if "%s%d" % job[1] in SORTED]
-        given = {"vector": 6, "scalar": 2}
-        filled = {}
-        waiting = []
-
-        def operands(job):
-            if job[0] == "project":
-                return [("X", job[1]), ("W", 0)]
-            if job[0] == "mix":
-                return [("P", 4 * (job[1] // 2) + job[2] // 2), ("K", 2 * job[1]), ("K", 2 * job[1] + 1)]
-            if job[0] in ("mix_half", "mix_row"):
-                return [("P", 4 * (job[1] // 2) + job[3] // 2), ("K", 2 * job[1]), ("K", 2 * job[1] + 1)]
-            return []
-
-        def emit_quantise(entry):
-            waiting.remove(entry)
-            quantise(*entry[1:])
-            given["vector"] += (entry[3] - entry[2]) / 512
-
-        for n, job in enumerate(jobs):
-            soon = [key for ahead in jobs[n:n + 2] for key in operands(ahead)]
-            for entry in list(waiting):
-                if entry[1] in soon:
-                    emit_quantise(entry)
-            if to_sort and to_sort[0] in jobs[n:n + SORT_LEAD + 1]:
-                sort(to_sort.pop(0)[1])
-                given["vector"] += 1
-            for entry in list(waiting):
-                if entry[0] <= given["vector"]:
-                    emit_quantise(entry)
-            kind = job[0]
-            on_vector = given["vector"] + (0 if kind.startswith("mix") else 0) <= given["scalar"] and n >= 8
-            if n >= len(jobs) - 7:
-                on_vector = (len(jobs) - n) % 2 == 0
-            engine = "vector" if on_vector else "scalar"
-            if kind != "turn_w":
-                given[engine] = max(given[engine], min(given.values())) + 1
-            ready = given[engine] + 0.5
-            if kind == "turn_w":
-                turn_w(job[1])
-                if job[1] == 1:
-                    waiting.append((0, ("W", 0), 0, 512))
-            elif kind == "turn":
-                turn(job[1], job[2], on_vector)
-                filled[job[1]] = max(filled.get(job[1], 0), ready)
-                if job[2] == 1:
-                    waiting.append((filled[job[1]], job[1], 0, 512))
-            elif kind == "project":
-                unit, h = job[1:]
-                project(unit, h, on_vector)
-                filled["K", unit] = max(filled.get(("K", unit), 0), ready)
-                heads = 2 if unit // 2 == PAIRS - 1 else NH
-                if (h + 1) % heads == 0:
-                    waiting.append((filled["K", unit], ("K", unit), (h + 1 - heads) * D, (h + 1) * D))
-            elif kind == "mix":
-                pair, j = job[1:]
-                mix(pair, j, on_vector)
-                rows = 2 if pair == PAIRS - 2 else 4
-                if (j + 1) % rows == 0:
-                    store(pair, 0, NH, j + 1 - rows, j + 1)
-            elif kind == "mix_row":
-                pair, h0, j = job[1:]
-                mix_row(pair, h0, j, on_vector)
-                if j % 2 == 1:
-                    store(pair, h0, h0 + 2, j + 1 - 2, j + 1)
-            else:
-                pair, h0, j0 = job[1:]
-                mix_half(pair, h0, j0, on_vector)
-                rows = 2 if n >= len(jobs) - 3 or (h0 == 0 and j0 < 4) else 4
-                if (j0 + 2) % rows == 0:
-                    store(pair, h0, h0 + 2, j0 + 2 - rows, j0 + 2)
+        widen(0)
+        widen(1)
+        steps = {"turn_w": turn_w, "turn": turn, "project": project, "mix": mix, "mix_head": mix_head, "quantise": quantise,
+                 "sort": sort, "vsort": vsort}
+        for job in jobs:
+            steps[job[0]](*job[1:])

@@ -50,7 +50,8 @@ def program():
         return banks([("mix", pair, j) for j in rows], engines)
 
     def mix_head(h, spans, engines):
-        return banks([("mix_head", h, j0, j1) for j0, j1 in spans], engines)
+        heads = 1 if h // 2 in QUARTERED else 2
+        return banks([("mix_part", LAST, h, heads, j0, j1, j0, j1) for j0, j1 in spans], engines)
 
     def quantise(keys):
         return [("quantise", key, 0, 512) for key in keys.split()]
@@ -67,17 +68,17 @@ def program():
     jobs = [("turn_w", 0), ("turn_w", 1)] + turn("X0 X1 P0", "SSSSSS")
     jobs += quantise_half("W0", 0) + quantise("X0") + quantise_half("W0", 1) + quantise("X1") + sort("X2 P1")
     jobs += project(0, range(4), "VSVS") + project(1, range(4), "VSVS")
-    jobs += quantise("P0 K0 K1") + turn("X2 P1", "SSSS") + quantise("X2") + vsort("X3") + quantise("P1") + sort("P3 X4") + turn("P2", "SV")
-    jobs += mix(0, (0, 1), "SV") + project(2, (0, 1), "SV") + mix(0, (2,), "S") + project(2, (2, 3), "VS") + quantise("P2") + mix(0, (3,), "S")
-    jobs += vsort("P5") + turn("X3 P3", "SVSS") + quantise("X3 P3") + sort("X5 P4") + turn("X4", "SV")
-    jobs += mix(0, (4, 5), "SV") + project(3, range(4), "SVSV") + quantise("X4 K2") + mix(0, (6, 7), "SS")
-    jobs += quantise("K3") + turn("X5 P5 P4", "SVSVSS") + quantise("X5 P5") + sort("X6 X7 P6")
+    jobs += quantise("P0 K0 K1") + turn("X2 P1", "SSSS") + quantise("X2") + vsort("X3") + quantise("P1") + sort("X4") + turn("P2", "SS")
+    jobs += mix(0, (0, 1), "VS") + project(2, (0, 1), "VV") + vsort("P3") + quantise("P2") + project(2, (2, 3), "SS") + mix(0, (2, 3), "SS")
+    jobs += turn("X3", "VS") + vsort("X5") + quantise("X3") + turn("P3", "SS") + vsort("P5") + quantise("P3") + sort("P4") + turn("X4", "SS")
+    jobs += mix(0, (4, 5), "VS") + project(3, range(4), "VSVS") + quantise("X4 K2") + mix(0, (6, 7), "SS")
+    jobs += quantise("K3") + turn("X5 P5 P4", "SVSSSS") + quantise("X5") + vsort("P7") + quantise("P4") + sort("X6 X7")
     jobs += project(4, (0, 1), "SV") + mix(1, (0,), "S") + project(4, (2, 3), "VS") + mix(1, (1, 2), "VS")
-    jobs += project(5, (0, 1), "SV") + mix(1, (3,), "S") + project(5, (2, 3), "VS") + mix(1, (4,), "V") + vsort("P7") + quantise("P4 K4 K5") + mix(1, (5, 6, 7), "SSS")
-    jobs += turn("X6 X7", "SVSS") + quantise("X6") + turn("P6", "VS") + quantise("X7") + turn("P7", "SS") + quantise("P6")
-    jobs += mix(2, (0, 1), "SV") + quantise("P7") + mix(2, (2,), "S") + both(0, "SV") + mix(2, (3,), "S") + both(1, "VS") + mix(2, (4, 5), "VS") + quantise("H0") + mix(2, (6, 7), "SV")
-    jobs += both(2, "SV") + mix_head(0, [(0, 2)], "S") + both(3, "VS") + quantise_half("H1", 0) + mix_head(0, [(2, 4), (4, 6)], "SV") + quantise_half("H1", 1) + mix_head(0, [(6, 8)], "S")
-    jobs += mix_head(2, [(0, 4), (4, 8)], "VV") + mix_head(3, [(0, 4), (4, 6), (6, 8)], "VSV")
+    jobs += project(5, (0, 1), "VS") + mix(1, (3,), "V") + project(5, (2, 3), "SV") + quantise("K4 P5 K5") + vsort("P6") + mix(1, (4, 5, 6, 7), "SSSS")
+    jobs += turn("X6 X7", "VSVS") + quantise("X6 X7") + turn("P7 P6", "SSVS")
+    jobs += mix(2, (0, 1), "VS") + quantise("P6") + mix(2, (2,), "S") + both(0, "VS") + quantise("P7") + mix(2, (3,), "S") + both(1, "VS") + mix(2, (4,), "V") + quantise("H0") + mix(2, (5, 6, 7), "SVS")
+    jobs += both(2, "VS") + mix_head(0, [(0, 2)], "V") + quantise_half("H1", 0) + both(3, "SS") + mix_head(0, [(2, 4), (4, 6)], "VS") + quantise_half("H1", 1) + mix_head(0, [(6, 8)], "V")
+    jobs += mix_head(2, [(0, 4), (4, 8)], "SV") + mix_head(3, [(0, 4), (4, 6), (6, 8)], "VSV")
     return jobs
 
 
@@ -255,28 +256,30 @@ def tile_causalselfattention_pa_t_kernel(tc, x, wk_bytes, wk_scale, pk_w, pk_b, 
                 nc.sync.dma_start(out=hbm_rows(pair)[:, :, j + 1 - rows:j + 1, :].rearrange("p h j d -> p h (j d)"),
                                   in_=otiles[pair][:].rearrange("p h j d -> p h (j d)"))
 
-        def mix_head(h, j0, j1, on_vector):
+        def mix_part(pair, h, heads, j0, j1, s0, s1, on_vector):
             rows = j1 - j0
-            heads = 1 if h // 2 in QUARTERED else 2
-            o = work.tile([P, heads, rows, D], F32, name="o", bufs=OBUFS, align_bytes=64)
+            if j0 == s0:
+                otiles[pair, h] = work.tile([P, heads, s1 - s0, D], F32, name="o", bufs=OBUFS, align_bytes=64)
+            o = otiles[pair, h]
             bank = psum.tile([P, 512], F32, name="bank")
             w = heads * D
             for jj in range(rows):
-                mix_passes(bank[:, jj * w:(jj + 1) * w], LAST, j0 + jj, h, heads)
+                mix_passes(bank[:, jj * w:(jj + 1) * w], pair, j0 + jj, h, heads)
             src = bank[:, 0:rows * w].rearrange("p (j h d) -> p j h d", h=heads, d=D)
-            dst = o[:].rearrange("p h j d -> p j h d")
-            columns = bias[:, LAST // 2, j0:j1]
+            dst = o[:, :, j0 - s0:j1 - s0, :].rearrange("p h j d -> p j h d")
+            columns = bias[:, pair // 2, j0:j1]
             if on_vector:
                 nc.vector.tensor_tensor(out=dst, in0=src, op=ADD, in1=columns.unsqueeze(2).unsqueeze(3).to_broadcast([P, rows, heads, D]))
             else:
                 for jj in range(rows):
                     nc.scalar.activation(out=dst[:, jj], in_=src[:, jj], func=IDENT, bias=columns[:, jj:jj + 1])
-            nc.sync.dma_start(out=hbm_rows(LAST)[:, h:h + heads, j0:j1, :].rearrange("p h j d -> p h (j d)"),
-                              in_=o[:].rearrange("p h j d -> p h (j d)"))
+            if j1 == s1:
+                nc.sync.dma_start(out=hbm_rows(pair)[:, h:h + heads, s0:s1, :].rearrange("p h j d -> p h (j d)"),
+                                  in_=o[:].rearrange("p h j d -> p h (j d)"))
 
         widen(0)
         widen(1)
-        steps = {"turn_w": turn_w, "turn": turn, "project": project, "mix": mix, "mix_head": mix_head, "quantise": quantise,
+        steps = {"turn_w": turn_w, "turn": turn, "project": project, "mix": mix, "mix_part": mix_part, "quantise": quantise,
                  "sort": sort, "vsort": vsort}
         for job in jobs:
             steps[job[0]](*job[1:])

@@ -35,7 +35,7 @@ QUARTERED = [1]
 def program():
     def banks(jobs, engines):
         assert len(jobs) == len(engines)
-        return [job + (e == "V",) for job, e in zip(jobs, engines)]
+        return [job + (e,) for job, e in zip(jobs, engines)]
 
     def turn(keys, engines):
         return banks([("turn", key, a) for key in keys.split() for a in range(2)], engines)
@@ -62,16 +62,19 @@ def program():
     def sort(keys):
         return [("sort", key, n == 0) for n, key in enumerate(keys.split())]
 
+    def late(n):
+        return [("late",)] * n
+
     def vsort(keys):
         return [("vsort", key) for key in keys.split()]
 
     jobs = [("turn_w", 0), ("turn_w", 1)] + turn("X0 X1 P0", "SSSSSS")
-    jobs += quantise_half("W0", 0) + quantise("X0") + quantise_half("W0", 1) + quantise("X1") + sort("X2 P1")
-    jobs += project(0, range(4), "VSVS") + project(1, range(4), "VSVS")
-    jobs += quantise("P0 K0 K1") + turn("X2 P1", "SSSS") + quantise("X2") + vsort("X3") + quantise("P1") + sort("X4") + turn("P2", "SS")
-    jobs += mix(0, (0, 1), "VS") + project(2, (0, 1), "VV") + vsort("P3") + quantise("P2") + project(2, (2, 3), "SS") + mix(0, (2, 3), "SS")
-    jobs += turn("X3", "VS") + vsort("X5") + quantise("X3") + turn("P3", "SS") + vsort("P5") + quantise("P3") + sort("P4") + turn("X4", "SS")
-    jobs += mix(0, (4, 5), "VS") + project(3, range(4), "VSVS") + quantise("X4 K2") + mix(0, (6, 7), "SS")
+    jobs += quantise_half("W0", 0) + quantise("X0") + quantise_half("W0", 1) + quantise("X1") + sort("X2")
+    jobs += project(0, range(4), "VSVS") + project(1, range(4), "VSSS")
+    jobs += vsort("P1") + quantise("P0 K0 K1") + turn("X2 P2", "SSVs") + turn("P1", "SS") + late(1) + quantise("X2") + vsort("X3") + quantise("P1") + sort("X4")
+    jobs += mix(0, (0, 1), "VS") + project(2, (0, 1), "VV") + vsort("P3") + quantise("P2") + project(2, (2, 3), "SS") + mix(0, (2, 3), "Sv")
+    jobs += vsort("X5") + turn("X3", "SS") + quantise("X3") + late(1) + turn("X4 P3", "vsSS") + quantise("P3") + sort("P4") + late(2)
+    jobs += mix(0, (4, 5), "VS") + project(3, range(4), "VSSS") + vsort("P5") + quantise("X4 K2") + mix(0, (6, 7), "SS")
     jobs += quantise("K3") + turn("X5 P5 P4", "SVSSSS") + quantise("X5") + vsort("P7") + quantise("P4") + sort("X6 X7")
     jobs += project(4, (0, 1), "SV") + mix(1, (0,), "S") + project(4, (2, 3), "VS") + mix(1, (1, 2), "VS")
     jobs += project(5, (0, 1), "VS") + mix(1, (3,), "V") + project(5, (2, 3), "SV") + quantise("K4 P5 K5") + vsort("P6") + mix(1, (4, 5, 6, 7), "SSSS")
@@ -88,7 +91,7 @@ def tile_causalselfattention_pa_t_kernel(tc, x, wk_bytes, wk_scale, pk_w, pk_b, 
     with ExitStack() as ctx:
         keep = ctx.enter_context(tc.tile_pool(name="keep", bufs=1))
         work = ctx.enter_context(tc.tile_pool(name="work", bufs=1))
-        psum = ctx.enter_context(tc.psum_pool(name="psum", bufs=BANKS))
+        psum = ctx.enter_context(tc.psum_pool(name="psum", bufs=1))
         ctx.enter_context(tc.manual_schedule())
 
         ws = keep.tile([P, 4], F32, name="ws", align_bytes=64)
@@ -146,11 +149,35 @@ def tile_causalselfattention_pa_t_kernel(tc, x, wk_bytes, wk_scale, pk_w, pk_b, 
             codes[key] = work.tile([P, 512 + 64], U32, name="codes" + kind, bufs=DEPTH[kind], align_bytes=256)[:, c0 // 4:c0 // 4 + 512]
             scales[key] = work.tile([P, 512 + 256], U8, name="scales" + kind, bufs=DEPTH[kind], align_bytes=256)[:, s0:s0 + 512]
 
-        def copy_out(on_vector, dst, src):
-            if on_vector:
-                nc.vector.tensor_copy(out=dst, in_=src)
+        held = []
+        free_banks = list(range(BANKS))
+        taken = []
+
+        def take_bank():
+            taken.append(free_banks.pop(0))
+            return psum.tile([P, 512], F32, name="bank%d" % taken[-1])
+
+        def empty(engine, call):
+            number = taken.pop()
+
+            def run():
+                call(engine in "Vv")
+                free_banks.append(number)
+            if engine in "VS":
+                run()
             else:
-                nc.scalar.copy(out=dst, in_=src)
+                held.append(run)
+
+        def late():
+            held.pop(0)()
+
+        def copy_out(engine, dst, src):
+            def call(on_vector):
+                if on_vector:
+                    nc.vector.tensor_copy(out=dst, in_=src)
+                else:
+                    nc.scalar.copy(out=dst, in_=src)
+            empty(engine, call)
 
         def widen(a):
             wv[a] = keep.tile([P, 2 * C], BF16, name="wv%d" % a, align_bytes=64)
@@ -177,7 +204,7 @@ def tile_causalselfattention_pa_t_kernel(tc, x, wk_bytes, wk_scale, pk_w, pk_b, 
                 new_operand(key)
             r = raw[key, a]
             src = words.get((key, a), [r[:, 256 * g + u:256 * (g + 1):2] for g in range(2) for u in range(2)])
-            bank = psum.tile([P, 512], F32, name="bank")
+            bank = take_bank()
             for n in range(4):
                 nc.tensor.transpose(bank[:, n * P:(n + 1) * P], src[n], ident[:])
             if a == 1 and ("sorted", key) in slot_of:
@@ -196,7 +223,7 @@ def tile_causalselfattention_pa_t_kernel(tc, x, wk_bytes, wk_scale, pk_w, pk_b, 
             key = "W0"
             if a == 0:
                 new_operand(key)
-            bank = psum.tile([P, 512], F32, name="bank")
+            bank = take_bank()
             ww = wv[a][:].bitcast(F32)
             for u in range(2):
                 for i in range(2):
@@ -207,6 +234,7 @@ def tile_causalselfattention_pa_t_kernel(tc, x, wk_bytes, wk_scale, pk_w, pk_b, 
                 in0=bank[:].bitcast(BF16).rearrange("p (u c e) -> p c u e", u=2, e=2),
                 in1=ws[:].rearrange("p (u e) -> p u e", e=2).unsqueeze(1).to_broadcast([P, 2 * P, 2, 2]),
                 op=MULT)
+            free_banks.append(taken.pop())
 
         def mx_pass(dst, stationary, s0, moving, m0, width, start, stop):
             nc.tensor.matmul_mx(
@@ -224,7 +252,7 @@ def tile_causalselfattention_pa_t_kernel(tc, x, wk_bytes, wk_scale, pk_w, pk_b, 
             key, c0 = keys_place(unit, h)
             if key not in grouped:
                 new_operand(key)
-            bank = psum.tile([P, 512], F32, name="bank")
+            bank = take_bank()
             for t in range(4):
                 mx_pass(bank[:, t * P:(t + 1) * P], "X%d" % unit, t * P, "W0", h * D, D, True, True)
             copy_out(on_vector, grouped[key][:, 4 * c0:4 * (c0 + D)].rearrange("p (n i t) -> p n t i", t=4, i=2),
@@ -243,43 +271,48 @@ def tile_causalselfattention_pa_t_kernel(tc, x, wk_bytes, wk_scale, pk_w, pk_b, 
             rows = STORE_ROWS[pair][j // 4]
             if j % rows == 0:
                 otiles[pair] = work.tile([P, NH, rows, D], F32, name="o", bufs=OBUFS, align_bytes=64)
-            bank = psum.tile([P, 512], F32, name="bank")
+            bank = take_bank()
             mix_passes(bank[:], pair, j, 0, NH)
             src = bank[:].rearrange("p (h d) -> p h d", h=NH)
             dst = otiles[pair][:, :, j % rows, :]
             column = bias[:, pair // 2, j:j + 1]
-            if on_vector:
-                nc.vector.tensor_scalar(out=dst, in0=src, scalar1=column, scalar2=None, op0=ADD)
-            else:
-                nc.scalar.activation(out=dst, in_=src, func=IDENT, bias=column)
-            if (j + 1) % rows == 0:
-                nc.sync.dma_start(out=hbm_rows(pair)[:, :, j + 1 - rows:j + 1, :].rearrange("p h j d -> p h (j d)"),
-                                  in_=otiles[pair][:].rearrange("p h j d -> p h (j d)"))
+            o = otiles[pair]
+
+            def call(vec):
+                if vec:
+                    nc.vector.tensor_scalar(out=dst, in0=src, scalar1=column, scalar2=None, op0=ADD)
+                else:
+                    nc.scalar.activation(out=dst, in_=src, func=IDENT, bias=column)
+                if (j + 1) % rows == 0:
+                    nc.sync.dma_start(out=hbm_rows(pair)[:, :, j + 1 - rows:j + 1, :].rearrange("p h j d -> p h (j d)"),
+                                      in_=o[:].rearrange("p h j d -> p h (j d)"))
+            empty(on_vector, call)
 
         def mix_part(pair, h, heads, j0, j1, s0, s1, on_vector):
             rows = j1 - j0
             if j0 == s0:
                 otiles[pair, h] = work.tile([P, heads, s1 - s0, D], F32, name="o", bufs=OBUFS, align_bytes=64)
             o = otiles[pair, h]
-            bank = psum.tile([P, 512], F32, name="bank")
+            bank = take_bank()
             w = heads * D
             for jj in range(rows):
                 mix_passes(bank[:, jj * w:(jj + 1) * w], pair, j0 + jj, h, heads)
             src = bank[:, 0:rows * w].rearrange("p (j h d) -> p j h d", h=heads, d=D)
             dst = o[:, :, j0 - s0:j1 - s0, :].rearrange("p h j d -> p j h d")
             columns = bias[:, pair // 2, j0:j1]
-            if on_vector:
+            if on_vector == "V":
                 nc.vector.tensor_tensor(out=dst, in0=src, op=ADD, in1=columns.unsqueeze(2).unsqueeze(3).to_broadcast([P, rows, heads, D]))
             else:
                 for jj in range(rows):
                     nc.scalar.activation(out=dst[:, jj], in_=src[:, jj], func=IDENT, bias=columns[:, jj:jj + 1])
+            free_banks.append(taken.pop())
             if j1 == s1:
                 nc.sync.dma_start(out=hbm_rows(pair)[:, h:h + heads, s0:s1, :].rearrange("p h j d -> p h (j d)"),
                                   in_=o[:].rearrange("p h j d -> p h (j d)"))
 
         widen(0)
         widen(1)
-        steps = {"turn_w": turn_w, "turn": turn, "project": project, "mix": mix, "mix_part": mix_part, "quantise": quantise,
+        steps = {"turn_w": turn_w, "turn": turn, "project": project, "mix": mix, "mix_part": mix_part, "late": late, "quantise": quantise,
                  "sort": sort, "vsort": vsort}
         for job in jobs:
             steps[job[0]](*job[1:])

@@ -27,8 +27,8 @@ SPLIT = ["X0"]
 BIAS_AFTER = 9
 SLOTS = 11
 DEPTH = {"W": 1, "X": 4, "P": 6, "K": 5}
-STORE_ROWS = [(4, 4), (4, 4), (2, 2)]
-OBUFS = 7
+STORE_ROWS = [(4, 4), (4, 2), (2, 2)]
+OBUFS = 8
 QUARTERED = [1]
 
 
@@ -71,17 +71,17 @@ def program():
     jobs = [("turn_w", 0), ("turn_w", 1)] + turn("X0 X1 P0", "SSSSSS")
     jobs += quantise_half("W0", 0) + quantise("X0") + quantise_half("W0", 1) + quantise("X1") + sort("X2")
     jobs += project(0, range(4), "VSVS") + project(1, range(4), "VSSS")
-    jobs += vsort("P1") + quantise("P0 K0 K1") + turn("X2 P2", "SSVs") + turn("P1", "SS") + late(1) + quantise("X2") + vsort("X3") + quantise("P1") + sort("X4")
-    jobs += mix(0, (0, 1), "VS") + project(2, (0, 1), "VV") + vsort("P3") + quantise("P2") + project(2, (2, 3), "SS") + mix(0, (2, 3), "Sv")
-    jobs += vsort("X5") + turn("X3", "SS") + quantise("X3") + late(1) + turn("X4 P3", "vsSS") + quantise("P3") + sort("P4") + late(2)
-    jobs += mix(0, (4, 5), "VS") + project(3, range(4), "VSSS") + vsort("P5") + quantise("X4 K2") + mix(0, (6, 7), "SS")
-    jobs += quantise("K3") + turn("X5 P5 P4", "SVSSSS") + quantise("X5") + vsort("P7") + quantise("P4") + sort("X6 X7")
-    jobs += project(4, (0, 1), "SV") + mix(1, (0,), "S") + project(4, (2, 3), "VS") + mix(1, (1, 2), "VS")
-    jobs += project(5, (0, 1), "VS") + mix(1, (3,), "V") + project(5, (2, 3), "SV") + quantise("K4 P5 K5") + vsort("P6") + mix(1, (4, 5, 6, 7), "SSSS")
-    jobs += turn("X6 X7", "VSVS") + quantise("X6 X7") + turn("P7 P6", "SSVS")
-    jobs += mix(2, (0, 1), "VS") + quantise("P6") + mix(2, (2,), "S") + both(0, "VS") + quantise("P7") + mix(2, (3,), "S") + both(1, "VS") + mix(2, (4,), "V") + quantise("H0") + mix(2, (5, 6, 7), "SVS")
-    jobs += both(2, "VS") + mix_head(0, [(0, 2)], "V") + quantise_half("H1", 0) + both(3, "SS") + mix_head(0, [(2, 4), (4, 6)], "VS") + quantise_half("H1", 1) + mix_head(0, [(6, 8)], "V")
-    jobs += mix_head(2, [(0, 4), (4, 8)], "SV") + mix_head(3, [(0, 4), (4, 6), (6, 8)], "VSV")
+    jobs += vsort("P1") + quantise("P0 K0 K1") + turn("X2 P2", "SSVs") + turn("P1", "SS") + late(1) + quantise("X2") + vsort("X3") + quantise("P1") + vsort("P3") + quantise("P2") + sort("X4")
+    jobs += mix(0, (0, 1), "SS") + project(2, range(4), "VSVS") + mix(0, (2,), "s")
+    jobs += turn("X3", "VS") + quantise("X3") + turn("P3", "SS") + late(1) + quantise("P3") + sort("X5")
+    jobs += mix(0, (3, 4, 5), "VSV") + project(3, range(4), "SVSS") + vsort("P4") + quantise("K2 K3") + mix(0, (6, 7), "Ss")
+    jobs += turn("X4 X5", "SSVS") + quantise("X4 X5") + sort("X6 X7") + late(1) + turn("P4", "SS")
+    jobs += mix(1, (0, 1), "VS") + project(4, range(4), "VSVS") + mix(1, (2, 3), "VS") + project(5, (0,), "V") + vsort("P5") + quantise("P4 K4") + project(5, (1, 2, 3), "SSS") + mix(1, (4, 5), "SS")
+    jobs += quantise("K5") + turn("X6 X7", "VSVS") + quantise("X6") + vsort("P6") + turn("P5", "SS") + quantise("X7 P5") + sort("P7")
+    jobs += mix(1, (6, 7), "SS") + mix(2, (0, 1), "vs") + both(0, "VS") + both(1, "VS") + late(2) + quantise("H0") + mix(2, (2, 3), "SS")
+    jobs += turn("P6 P7", "VSVS") + quantise_half("P6", 0) + quantise_half("P6", 1) + quantise_half("P7", 0) + quantise_half("P7", 1) + mix_head(0, [(0, 2), (2, 4)], "SV")
+    jobs += mix(2, (4, 5, 6, 7), "SVSV") + both(2, "SV") + quantise_half("H1", 0) + both(3, "SS") + mix_head(0, [(4, 6)], "V") + quantise_half("H1", 1) + mix_head(0, [(6, 8)], "S")
+    jobs += mix_head(2, [(0, 4), (4, 8)], "VV") + mix_head(3, [(0, 4), (4, 8)], "VV")
     return jobs
 
 
@@ -94,14 +94,14 @@ def tile_causalselfattention_pa_t_kernel(tc, x, wk_bytes, wk_scale, pk_w, pk_b, 
         psum = ctx.enter_context(tc.psum_pool(name="psum", bufs=1))
         ctx.enter_context(tc.manual_schedule())
 
-        ws = keep.tile([P, 4], F32, name="ws", align_bytes=64)
-        nc.scalar.dma_start(out=ws[:], in_=wk_scale.rearrange("o (p t) -> p (o t)", t=4))
+        ws = keep.tile([P, 2, 4], F32, name="ws", align_bytes=64)
+        nc.scalar.dma_start(out=ws[:], in_=wk_scale.rearrange("o (p t) -> p o t", t=4).to_broadcast([P, 2, 4]))
 
         wb, raw, whole = {}, {}, {}
 
         def load_w(a):
             wb[a] = keep.tile([P, 2, C], U8, name="wb%d" % a, align_bytes=64)
-            nc.sync.dma_start(out=wb[a][:], in_=wk_bytes.rearrange("(h r) k -> r h k", h=NH)[:, 2 * a:2 * a + 2, :])
+            nc.sync.dma_start(out=wb[a][:], in_=wk_bytes.rearrange("(a r i) k -> a r i k", a=2, i=2)[a])
 
         def load(key, pieces):
             kind, i = key[0], int(key[1])
@@ -225,14 +225,14 @@ def tile_causalselfattention_pa_t_kernel(tc, x, wk_bytes, wk_scale, pk_w, pk_b, 
                 new_operand(key)
             bank = take_bank()
             ww = wv[a][:].bitcast(F32)
-            for u in range(2):
-                for i in range(2):
-                    n = 2 * u + i
+            for i in range(2):
+                for u in range(2):
+                    n = 2 * i + u
                     nc.tensor.transpose(bank[:, n * P:(n + 1) * P], ww[:, 256 * i + u:256 * (i + 1):2], ident[:])
             nc.vector.tensor_tensor(
-                out=grouped[key][:, a * 1024:(a + 1) * 1024].rearrange("p (c u e) -> p c u e", u=2, e=2),
-                in0=bank[:].bitcast(BF16).rearrange("p (u c e) -> p c u e", u=2, e=2),
-                in1=ws[:].rearrange("p (u e) -> p u e", e=2).unsqueeze(1).to_broadcast([P, 2 * P, 2, 2]),
+                out=grouped[key][:, a * 1024:(a + 1) * 1024].rearrange("p (r n e) -> p r n e", n=4, e=2),
+                in0=bank[:].bitcast(BF16).rearrange("p (n r e) -> p r n e", n=4, e=2),
+                in1=ws[:].rearrange("p i (u e) -> p (i u) e", e=2).unsqueeze(1).to_broadcast([P, P, 4, 2]),
                 op=MULT)
             free_banks.append(taken.pop())
 

from contextlib import ExitStack

import concourse.mybir as mybir
from concourse.masks import make_identity

B, T, C, NH, NC = 2, 2048, 512, 4, 2
D = C // NH
N = T // NC
FLOPS = 2 * B * T * C * C + 2 * B * T * N * C

F32 = mybir.dt.float32
BF16 = mybir.dt.bfloat16
U32 = mybir.dt.uint32
U8 = mybir.dt.uint8
FP8 = mybir.dt.float8_e4m3fn
FP8X4 = mybir.dt.float8_e4m3fn_x4
ADD = mybir.AluOpType.add
MULT = mybir.AluOpType.mult
IDENT = mybir.ActivationFunctionType.Identity

P = 128
BANKS = 8
ROWS = N // P
PAIRS = B * NC
LAST = PAIRS - 1
SPLIT = ["X0"]
BIAS_AFTER = 9
SLOTS = 11
DEPTH = {"W": 1, "X": 4, "P": 6, "K": 5}
STORE_ROWS = [(4, 4), (4, 2), (2, 2)]
OBUFS = 8
QUARTERED = [1]


def program():
    def banks(jobs, engines):
        assert len(jobs) == len(engines)
        return [job + (e,) for job, e in zip(jobs, engines)]

    def turn(keys, engines):
        return banks([("turn", key, a) for key in keys.split() for a in range(2)], engines)

    def project(unit, heads, engines):
        return banks([("project", unit, h) for h in heads], engines)

    def both(h, engines):
        return banks([("project", 2 * LAST + u, h) for u in range(2)], engines)

    def mix(pair, rows, engines):
        return banks([("mix", pair, j) for j in rows], engines)

    def mix_head(h, spans, engines):
        heads = 1 if h // 2 in QUARTERED else 2
        return banks([("mix_part", LAST, h, heads, j0, j1, j0, j1) for j0, j1 in spans], engines)

    def quantise(keys):
        return [("quantise", key, 0, 512) for key in keys.split()]

    def quantise_half(key, a):
        return [("quantise", key, 256 * a, 256 * (a + 1))]

    def sort(keys):
        return [("sort", key, n == 0) for n, key in enumerate(keys.split())]

    def late(n):
        return [("late",)] * n

    def vsort(keys):
        return [("vsort", key) for key in keys.split()]

    jobs = [("turn_w", 0), ("turn_w", 1)] + turn("X0 X1 P0", "SSSSSS")
    jobs += quantise_half("W0", 0) + quantise("X0") + quantise_half("W0", 1) + quantise("X1") + sort("X2")
    jobs += project(0, range(4), "VSVS") + project(1, range(4), "VSSS")
    jobs += vsort("P1") + quantise("P0 K0 K1") + turn("X2 P2", "SSVs") + turn("P1", "SS") + late(1) + quantise("X2") + vsort("X3") + quantise("P1") + vsort("P3") + quantise("P2") + sort("X4")
    jobs += mix(0, (0, 1), "SS") + project(2, range(4), "VSVS") + mix(0, (2,), "s")
    jobs += turn("X3", "VS") + quantise("X3") + turn("P3", "SS") + late(1) + quantise("P3") + sort("X5")
    jobs += mix(0, (3, 4, 5), "VSV") + project(3, range(4), "SVSS") + vsort("P4") + quantise("K2 K3") + mix(0, (6, 7), "Ss")
    jobs += turn("X4 X5", "SSVS") + quantise("X4 X5") + sort("X6 X7") + late(1) + turn("P4", "SS")
    jobs += mix(1, (0, 1), "VS") + project(4, range(4), "VSVS") + mix(1, (2, 3), "VS") + project(5, (0,), "V") + vsort("P5") + quantise("P4 K4") + project(5, (1, 2, 3), "SSS") + mix(1, (4, 5), "SS")
    jobs += quantise("K5") + turn("X6 X7", "VSVS") + quantise("X6") + vsort("P6") + turn("P5", "SS") + quantise("X7 P5") + sort("P7")
    jobs += mix(1, (6, 7), "SS") + mix(2, (0, 1), "vs") + both(0, "VS") + both(1, "VS") + late(2) + quantise("H0") + mix(2, (2, 3), "SS")
    jobs += turn("P6 P7", "VSVS") + quantise_half("P6", 0) + quantise_half("P6", 1) + quantise_half("P7", 0) + quantise_half("P7", 1) + mix_head(0, [(0, 2), (2, 4)], "SV")
    jobs += mix(2, (4, 5, 6, 7), "SVSV") + both(2, "SV") + quantise_half("H1", 0) + both(3, "SS") + mix_head(0, [(4, 6)], "V") + quantise_half("H1", 1) + mix_head(0, [(6, 8)], "S")
    jobs += mix_head(2, [(0, 4), (4, 8)], "VV") + mix_head(3, [(0, 4), (4, 8)], "VV")
    return jobs


def tile_causalselfattention_pa_t_kernel(tc, x, wk_bytes, wk_scale, pk_w, pk_b, out):
    nc = tc.nc
    jobs = program()
    with ExitStack() as ctx:
        keep = ctx.enter_context(tc.tile_pool(name="keep", bufs=1))
        work = ctx.enter_context(tc.tile_pool(name="work", bufs=1))
        psum = ctx.enter_context(tc.psum_pool(name="psum", bufs=1))
        ctx.enter_context(tc.manual_schedule())

        ws = keep.tile([P, 2, 4], F32, name="ws", align_bytes=64)
        nc.scalar.dma_start(out=ws[:], in_=wk_scale.rearrange("o (p t) -> p o t", t=4).to_broadcast([P, 2, 4]))

        wb, raw, whole = {}, {}, {}

        def load_w(a):
            wb[a] = keep.tile([P, 2, C], U8, name="wb%d" % a, align_bytes=64)
            nc.sync.dma_start(out=wb[a][:], in_=wk_bytes.rearrange("(a r i) k -> a r i k", a=2, i=2)[a])

        def load(key, pieces):
            kind, i = key[0], int(key[1])
            if kind == "X":
                c, b, u = i // 4, i // 2 % 2, i % 2
                r0 = c * N + u * 512
                src = x[b, r0:r0 + 512, :].rearrange("(m t) k -> m (t k)", t=4)
            else:
                c, q = divmod(i, 4)
                src = pk_w[c].rearrange("(m j) k -> m (j k)", j=ROWS)[:, 2 * q * N:2 * (q + 1) * N]
            w = 2048 // pieces
            for s in range(pieces):
                t = keep.tile([P, w], BF16, name="raw%s%d_%d" % (kind, i, s), align_bytes=64)
                nc.sync.dma_start(out=t[:], in_=src[:, s * w:(s + 1) * w])
                whole[key] = t[:].bitcast(F32)
                for a in range(2 // pieces):
                    raw[key, s + a] = t[:, a * 1024:(a + 1) * 1024].bitcast(F32)

        bias = keep.tile([P, NC, ROWS], BF16, name="bias", align_bytes=64)
        loads = [job for job in jobs if job[0] == "turn_w" or job[0] == "turn" and job[2] == 0]
        load_w(0)
        load_w(1)
        for n, job in enumerate(loads):
            if job[0] != "turn_w":
                load(job[1], 2 if job[1] in SPLIT else 1)
            if n == BIAS_AFTER:
                nc.sync.dma_start(out=bias[:], in_=pk_b.rearrange("c (p j) -> p c j", j=ROWS))

        ident = keep.tile([P, P], F32, name="ident", align_bytes=64)
        make_identity(nc, ident[:])

        grouped, codes, scales, words, otiles, wv = {}, {}, {}, {}, {}, {}
        free_slots = list(range(SLOTS))
        slot_of = {}

        def take_slot(owner, shape, dtype, newest):
            slot_of[owner] = free_slots.pop(-1 if newest else 0)
            return work.tile(shape, dtype, name="slot%d" % slot_of[owner], align_bytes=64)

        def new_operand(key):
            grouped[key] = take_slot(key, [P, 2048], BF16, False)[:]
            moving = key[0] in "WKH"
            c0, s0 = (0, 64) if moving else (128, 192)
            kind = "K" if key[0] == "H" else key[0]
            codes[key] = work.tile([P, 512 + 64], U32, name="codes" + kind, bufs=DEPTH[kind], align_bytes=256)[:, c0 // 4:c0 // 4 + 512]
            scales[key] = work.tile([P, 512 + 256], U8, name="scales" + kind, bufs=DEPTH[kind], align_bytes=256)[:, s0:s0 + 512]

        held = []
        free_banks = list(range(BANKS))
        taken = []

        def take_bank():
            taken.append(free_banks.pop(0))
            return psum.tile([P, 512], F32, name="bank%d" % taken[-1])

        def empty(engine, call):
            number = taken.pop()

            def run():
                call(engine in "Vv")
                free_banks.append(number)
            if engine in "VS":
                run()
            else:
                held.append(run)

        def late():
            held.pop(0)()

        def copy_out(engine, dst, src):
            def call(on_vector):
                if on_vector:
                    nc.vector.tensor_copy(out=dst, in_=src)
                else:
                    nc.scalar.copy(out=dst, in_=src)
            empty(engine, call)

        def widen(a):
            wv[a] = keep.tile([P, 2 * C], BF16, name="wv%d" % a, align_bytes=64)
            nc.vector.tensor_copy(out=wv[a][:], in_=wb[a][:].rearrange("p i k -> p (i k)").bitcast(FP8))

        def sorted_tile(key, newest):
            d = take_slot(("sorted", key), [P, 8, P], F32, newest)
            for a in range(2):
                words[key, a] = [d[:, 4 * a + n, :] for n in range(4)]
            return d

        def sort(key, first):
            d = sorted_tile(key, first)
            nc.gpsimd.tensor_copy(out=d[:].rearrange("p (g u) m -> p g u m", u=2),
                                  in_=whole[key].rearrange("p (g m u) -> p g u m", g=4, u=2))

        def vsort(key):
            d = sorted_tile(key, False)
            nc.vector.tensor_copy(out=d[:].rearrange("p (g u) (m i) -> p g m u i", u=2, i=4),
                                  in_=whole[key].rearrange("p (g m i u) -> p g m u i", g=4, u=2, i=4))

        def turn(key, a, on_vector):
            if a == 0:
                new_operand(key)
            r = raw[key, a]
            src = words.get((key, a), [r[:, 256 * g + u:256 * (g + 1):2] for g in range(2) for u in range(2)])
            bank = take_bank()
            for n in range(4):
                nc.tensor.transpose(bank[:, n * P:(n + 1) * P], src[n], ident[:])
            if a == 1 and ("sorted", key) in slot_of:
                free_slots.append(slot_of["sorted", key])
            copy_out(on_vector,
                     grouped[key][:, a * 1024:(a + 1) * 1024].bitcast(F32).rearrange("p (g m i u) -> p g m u i", g=2, u=2, i=2),
                     bank[:].rearrange("p (g u m i) -> p g m u i", g=2, u=2, i=2))

        def quantise(key, c0, c1):
            nc.vector.quantize_mx(out=codes[key][:, c0:c1].bitcast(FP8X4), scales=scales[key][:, c0:c1],
                                  in_=grouped[key][:, 4 * c0:4 * c1])
            if c1 == 512:
                free_slots.append(slot_of[key])

        def turn_w(a):
            key = "W0"
            if a == 0:
                new_operand(key)
            bank = take_bank()
            ww = wv[a][:].bitcast(F32)
            for i in range(2):
                for u in range(2):
                    n = 2 * i + u
                    nc.tensor.transpose(bank[:, n * P:(n + 1) * P], ww[:, 256 * i + u:256 * (i + 1):2], ident[:])
            nc.vector.tensor_tensor(
                out=grouped[key][:, a * 1024:(a + 1) * 1024].rearrange("p (r n e) -> p r n e", n=4, e=2),
                in0=bank[:].bitcast(BF16).rearrange("p (n r e) -> p r n e", n=4, e=2),
                in1=ws[:].rearrange("p i (u e) -> p (i u) e", e=2).unsqueeze(1).to_broadcast([P, P, 4, 2]),
                op=MULT)
            free_banks.append(taken.pop())

        def mx_pass(dst, stationary, s0, moving, m0, width, start, stop):
            nc.tensor.matmul_mx(
                out=dst,
                lhsT=codes[stationary][:, s0:s0 + P].bitcast(FP8X4), lhsT_scale=scales[stationary][:, s0:s0 + P],
                rhs=codes[moving][:, m0:m0 + width].bitcast(FP8X4), rhs_scale=scales[moving][:, m0:m0 + width],
                start=start, stop=stop)

        def keys_place(unit, h):
            if unit // 2 == LAST:
                return "H%d" % (h // 2), ((h % 2 * 2 + unit % 2) if h // 2 in QUARTERED else (unit % 2 * 2 + h % 2)) * D
            return "K%d" % unit, h * D

        def project(unit, h, on_vector):
            key, c0 = keys_place(unit, h)
            if key not in grouped:
                new_operand(key)
            bank = take_bank()
            for t in range(4):
                mx_pass(bank[:, t * P:(t + 1) * P], "X%d" % unit, t * P, "W0", h * D, D, True, True)
            copy_out(on_vector, grouped[key][:, 4 * c0:4 * (c0 + D)].rearrange("p (n i t) -> p n t i", t=4, i=2),
                     bank[:].rearrange("p (t n i) -> p n t i", t=4, i=2))

        def mix_passes(dst, pair, j, h, heads):
            for u in range(2):
                key, c0 = keys_place(2 * pair + u, h)
                mx_pass(dst, "P%d" % (4 * (pair // 2) + j // 2), (j % 2) * 256 + u * P, key, c0, heads * D, u == 0, u == 1)

        def hbm_rows(pair):
            c, b = divmod(pair, 2)
            return out[b, :, c * N:(c + 1) * N, :].rearrange("h (p j) d -> p h j d", j=ROWS)

        def mix(pair, j, on_vector):
            rows = STORE_ROWS[pair][j // 4]
            if j % rows == 0:
                otiles[pair] = work.tile([P, NH, rows, D], F32, name="o", bufs=OBUFS, align_bytes=64)
            bank = take_bank()
            mix_passes(bank[:], pair, j, 0, NH)
            src = bank[:].rearrange("p (h d) -> p h d", h=NH)
            dst = otiles[pair][:, :, j % rows, :]
            column = bias[:, pair // 2, j:j + 1]
            o = otiles[pair]

            def call(vec):
                if vec:
                    nc.vector.tensor_scalar(out=dst, in0=src, scalar1=column, scalar2=None, op0=ADD)
                else:
                    nc.scalar.activation(out=dst, in_=src, func=IDENT, bias=column)
                if (j + 1) % rows == 0:
                    nc.sync.dma_start(out=hbm_rows(pair)[:, :, j + 1 - rows:j + 1, :].rearrange("p h j d -> p h (j d)"),
                                      in_=o[:].rearrange("p h j d -> p h (j d)"))
            empty(on_vector, call)

        def mix_part(pair, h, heads, j0, j1, s0, s1, on_vector):
            rows = j1 - j0
            if j0 == s0:
                otiles[pair, h] = work.tile([P, heads, s1 - s0, D], F32, name="o", bufs=OBUFS, align_bytes=64)
            o = otiles[pair, h]
            bank = take_bank()
            w = heads * D
            for jj in range(rows):
                mix_passes(bank[:, jj * w:(jj + 1) * w], pair, j0 + jj, h, heads)
            src = bank[:, 0:rows * w].rearrange("p (j h d) -> p j h d", h=heads, d=D)
            dst = o[:, :, j0 - s0:j1 - s0, :].rearrange("p h j d -> p j h d")
            columns = bias[:, pair // 2, j0:j1]
            if on_vector == "V":
                nc.vector.tensor_tensor(out=dst, in0=src, op=ADD, in1=columns.unsqueeze(2).unsqueeze(3).to_broadcast([P, rows, heads, D]))
            else:
                for jj in range(rows):
                    nc.scalar.activation(out=dst[:, jj], in_=src[:, jj], func=IDENT, bias=columns[:, jj:jj + 1])
            free_banks.append(taken.pop())
            if j1 == s1:
                nc.sync.dma_start(out=hbm_rows(pair)[:, h:h + heads, s0:s1, :].rearrange("p h j d -> p h (j d)"),
                                  in_=o[:].rearrange("p h j d -> p h (j d)"))

        widen(0)
        widen(1)
        steps = {"turn_w": turn_w, "turn": turn, "project": project, "mix": mix, "mix_part": mix_part, "late": late, "quantise": quantise,
                 "sort": sort, "vsort": vsort}
        for job in jobs:
            steps[job[0]](*job[1:])
